import numpy as np
import ml_dtypes


def mxq(x, axis, fmt="e4m3"):
    dtype, down = {"e4m3": (ml_dtypes.float8_e4m3fn, 7), "e5m2": (ml_dtypes.float8_e5m2, 14)}[fmt]
    v = np.moveaxis(np.asarray(x, np.float32).astype(ml_dtypes.bfloat16).astype(np.float64), axis, -1)
    blocks = v.reshape(v.shape[:-1] + (-1, 32))
    amax = np.abs(blocks).max(-1, keepdims=True)
    byte = np.maximum(np.where(amax > 0, np.frexp(amax)[1] - 1 + 127, 0) - down, 1)
    scale = np.exp2(byte - 127.0)
    codes = (blocks / scale).astype(np.float32).astype(dtype).astype(np.float64)
    return np.moveaxis((codes * scale).reshape(v.shape), -1, axis)


WIDE = False


def mx_kscale(k):
    if not WIDE:
        return np.ones(k)
    levels = np.array([10, -10, 5, -5, 0])
    a = np.random.permutation(np.resize(levels, k // 512 * 4)).reshape(k // 512, 4)
    idx = np.arange(k)
    return np.exp2(a[idx // 512, idx % 128 // 32])


BF16 = ml_dtypes.bfloat16


def bf(x):
    return np.asarray(x, np.float32).astype(BF16)


def f64(x):
    return np.asarray(x).astype(np.float64)


E2M1 = np.array([0.0, 0.5, 1.0, 1.5, 2.0, 3.0, 4.0, 6.0, -0.0, -0.5, -1.0, -1.5, -2.0, -3.0, -4.0, -6.0])


def pack_weight(w, fmt):
    k, n = w.shape
    w = f64(bf(w)).reshape(k // 32, 32, n)
    amax = np.abs(w).max(1)
    if fmt == "e4m3":
        byte = np.frexp(amax)[1] - 1 + 127 - 7
    else:
        mant, ex = np.frexp(amax / 6.0)
        byte = np.where(mant > 0.5, ex, ex - 1) + 127
    byte = np.clip(np.where(amax > 0, byte, 1), 1, 254)
    scaled = (w * np.exp2(127.0 - byte)[:, None, :]).reshape(k, n).astype(np.float32)
    by_word = np.ascontiguousarray(scaled.reshape(k // 512, 128, 4, n).transpose(0, 1, 3, 2))
    if fmt == "e4m3":
        words = by_word.astype(ml_dtypes.float8_e4m3fn).view(np.uint8)
    else:
        c = by_word.astype(ml_dtypes.float4_e2m1fn).view(np.uint8) & 0xF
        words = c[..., 0::2] | (c[..., 1::2] << 4)
    return np.ascontiguousarray(words), np.ascontiguousarray(byte.astype(np.uint8).reshape(k // 512, 16, n))


def unpack_weight(words, scales, fmt):
    g, p, n, _ = words.shape
    if fmt == "e4m3":
        vals = np.ascontiguousarray(words).view(ml_dtypes.float8_e4m3fn).astype(np.float64)
    else:
        nib = np.empty((g, p, n, 4), np.uint8)
        nib[..., 0::2] = words & 0xF
        nib[..., 1::2] = words >> 4
        vals = E2M1[nib]
    vals = vals * np.repeat(np.exp2(scales.astype(np.float64) - 127.0), 8, axis=1)[..., None]
    return vals.transpose(0, 1, 3, 2).reshape(g * 512, n)


B, S, D, O, BS = 2, 256, 4096, 2048, 1024
MULT = D // BS


def fwht(x):
    n = x.shape[-1]
    steps = int(round(np.log2(n)))
    shape = x.shape
    x = x.reshape(-1, n)
    h = 1
    for _ in range(steps):
        x = x.reshape(-1, n // (2 * h), 2, h)
        a = x[:, :, 0, :]
        b = x[:, :, 1, :]
        x = np.stack([a + b, a - b], axis=2).reshape(-1, n)
        h *= 2
    return x.reshape(shape)


def pad_to_block_last(x, blocksize):
    size = x.shape[-1]
    target = ((size - 1) // blocksize + 1) * blocksize
    delta = target - size
    if delta == 0:
        return x
    pad = [(0, 0)] * (x.ndim - 1) + [(0, delta)]
    return np.pad(x, pad)


def block_factors():
    lv = np.unique(mx_kscale(D))
    lv = lv[np.argsort(-np.abs(np.log2(lv)), kind="stable")]
    return np.repeat(lv[np.arange(MULT) % len(lv)], BS)


def setup_inputs():
    s = block_factors()
    input = bf(np.random.standard_normal((B, S, D)) * s)
    weight = np.random.standard_normal((O, D)) / np.sqrt(D) / s[None, :]
    words, scales = pack_weight(np.ascontiguousarray(weight.T), "e4m3")
    return {"input": input, "weight_words": words, "weight_scales": scales}


def reference(input, weight_words, weight_scales):
    x = pad_to_block_last(f64(input), BS)
    lead = x.shape[:-1]
    d = x.shape[-1]
    mult = d // BS
    x = x.reshape(lead + (mult, BS))
    x = fwht(x) * (1.0 / np.sqrt(BS))
    x = x.reshape(lead + (d,))
    return mxq(x, 2, "e4m3") @ unpack_weight(weight_words, weight_scales, "e4m3")

@@ -1,0 +1,231 @@
+from contextlib import ExitStack
+
+import concourse.masks as masks
+import concourse.mybir as mybir
+
+F32 = mybir.dt.float32
+BF16 = mybir.dt.bfloat16
+I32 = mybir.dt.int32
+U32 = mybir.dt.uint32
+U8 = mybir.dt.uint8
+FP8X4 = mybir.dt.float8_e4m3fn_x4
+ALU = mybir.AluOpType
+
+P = 128
+TOKENS = 512
+FEATURES = 4096
+OUTPUTS = 2048
+BLOCK = 1024
+K_PASS = 512
+GROUPS = FEATURES // K_PASS
+N_TILE = 512
+N_TILES = OUTPUTS // N_TILE
+BLOCKS = FEATURES // BLOCK
+UNITS = (TOKENS // P) * BLOCKS
+PLANES_PER_TILE = 4
+SCALE = 1.0 / 32.0
+
+FLOPS = 2 * TOKENS * FEATURES * OUTPUTS + 10 * TOKENS * FEATURES
+
+
+def tile_hadlinear_kernel(tc, x, weight_words, weight_scales, out):
+    nc = tc.nc
+    x_rows = x.flatten_outer_dims()
+    out_rows = out.flatten_outer_dims()
+
+    with ExitStack() as ctx:
+        const = ctx.enter_context(tc.tile_pool(name="const", bufs=1))
+        x_pool = ctx.enter_context(tc.tile_pool(name="x_pool", bufs=UNITS))
+        w_pool = ctx.enter_context(tc.tile_pool(name="w_pool", bufs=GROUPS))
+        work = ctx.enter_context(tc.tile_pool(name="work", bufs=2))
+        ahead = ctx.enter_context(tc.tile_pool(name="ahead", bufs=3))
+        store_pool = ctx.enter_context(tc.tile_pool(name="store_pool", bufs=2 * N_TILES))
+        t_psum = ctx.enter_context(tc.psum_pool(name="t_psum", bufs=1))
+        even_psum = ctx.enter_context(tc.psum_pool(name="even_psum", bufs=2))
+        odd_psum = ctx.enter_context(tc.psum_pool(name="odd_psum", bufs=1))
+        acc_psum = ctx.enter_context(tc.psum_pool(name="acc_psum", bufs=1))
+        ctx.enter_context(tc.manual_schedule())
+
+        x_chunk = {}
+        w_words = {}
+
+        def load_x(unit):
+            tile_index, block = divmod(unit, BLOCKS)
+            x_chunk[unit] = x_pool.tile([P, BLOCK], BF16, name="x_chunk")
+            nc.sync.dma_start(
+                out=x_chunk[unit][:],
+                in_=x_rows[P * tile_index : P * (tile_index + 1), BLOCK * block : BLOCK * (block + 1)],
+            )
+
+        def load_w(g):
+            w_words[g] = w_pool.tile([P, OUTPUTS], U32, name="w_words", align_bytes=64)
+            nc.sync.dma_start(
+                out=w_words[g][:].bitcast(I32),
+                in_=weight_words[g].rearrange("p n t -> p (n t)").bitcast(I32),
+            )
+
+        w_planes = const.tile([P, GROUPS // PLANES_PER_TILE, OUTPUTS], U8, align_bytes=64)
+        nc.vector.memset(w_planes[:].rearrange("p a n -> p (a n)").bitcast(I32), 0)
+
+        for unit in range(BLOCKS):
+            load_x(unit)
+        for a in range(GROUPS // PLANES_PER_TILE):
+            for quadrant in range(4):
+                nc.sync.dma_start(
+                    out=w_planes[32 * quadrant : 32 * quadrant + 16, a, :].bitcast(I32),
+                    in_=weight_scales[
+                        PLANES_PER_TILE * a : PLANES_PER_TILE * (a + 1), 4 * quadrant : 4 * quadrant + 4, :
+                    ].bitcast(I32),
+                )
+        for g in range(GROUPS):
+            load_w(g)
+            load_x(BLOCKS + g)
+        for unit in range(BLOCKS + GROUPS, UNITS):
+            load_x(unit)
+
+        warm = const.tile([P, 1], F32)
+        nc.gpsimd.memset(warm[:], 0.0)
+        nc.scalar.mul(out=warm[:], in_=warm[:], mul=SCALE)
+
+        row_index = const.tile([P, P], I32)
+        col_index = const.tile([P, P], I32)
+        nc.gpsimd.iota(row_index[:], pattern=[[0, P]], base=0, channel_multiplier=1)
+        nc.gpsimd.iota(col_index[:], pattern=[[1, P]], base=0, channel_multiplier=0)
+        identity = const.tile([P, P], F32)
+        masks.make_identity(nc, identity[:])
+        bits = const.tile([P, P], I32)
+        nc.vector.tensor_tensor(out=bits[:], in0=row_index[:], in1=col_index[:], op=ALU.bitwise_and)
+        for shift in (4, 2, 1):
+            nc.vector.scalar_tensor_tensor(
+                out=bits[:],
+                in0=bits[:],
+                scalar=shift,
+                in1=bits[:],
+                op0=ALU.logical_shift_right,
+                op1=ALU.bitwise_xor,
+            )
+        nc.vector.tensor_single_scalar(out=bits[:], in_=bits[:], scalar=1, op=ALU.bitwise_and)
+        hadamard = const.tile([P, P], BF16)
+        nc.vector.tensor_scalar(
+            out=hadamard[:], in0=bits[:], scalar1=-2.0, scalar2=1.0, op0=ALU.mult, op1=ALU.add
+        )
+
+        x_t = {}
+        z_even = {}
+        z_odd_sb = {}
+        after_odd = {}
+        after_pair = {}
+        grouped = {}
+        y_codes = {}
+        y_scales = {}
+        acc = {}
+
+        def transpose_unit(unit):
+            words = x_chunk[unit][:].bitcast(F32)
+            t_bank = t_psum.tile([P, 4, P], F32, name="t_bank")
+            for pair in range(2):
+                for half in range(2):
+                    nc.tensor.transpose(
+                        t_bank[:, 2 * pair + half, :],
+                        words[:, 256 * half + pair : 256 * (half + 1) : 2],
+                        identity[:],
+                    )
+            x_t[unit] = ahead.tile([P, BLOCK], BF16, name="x_t")
+            nc.scalar.copy(out=x_t[unit][:].bitcast(F32), in_=t_bank[:].rearrange("p s k -> p (s k)"))
+
+        def hadamard_over_partitions(unit):
+            columns = x_t[unit][:].rearrange("p (w e) -> p w e", e=2)
+            z_odd = odd_psum.tile([P, 4 * P], F32, name="z_odd")
+            z_even[unit] = even_psum.tile([P, 4 * P], F32, name="z_even")
+            nc.tensor.matmul(out=z_odd[:], lhsT=hadamard[:], rhs=columns[:, :, 1], start=True, stop=True)
+            nc.tensor.matmul(out=z_even[unit][:], lhsT=hadamard[:], rhs=columns[:, :, 0], start=True, stop=True)
+            z_odd_sb[unit] = ahead.tile([P, 4 * P], F32, name="z_odd_sb")
+            nc.scalar.mul(out=z_odd_sb[unit][:], in_=z_odd[:], mul=SCALE)
+
+        def butterfly_odd(unit):
+            after_odd[unit] = work.tile([P, 2, 4 * P], F32, name="after_odd")
+            for sign, op in enumerate((ALU.add, ALU.subtract)):
+                nc.vector.scalar_tensor_tensor(
+                    out=after_odd[unit][:, sign, :],
+                    in0=z_even[unit][:],
+                    scalar=SCALE,
+                    in1=z_odd_sb[unit][:],
+                    op0=ALU.mult,
+                    op1=op,
+                )
+
+        def butterfly_pair(unit):
+            planes = after_odd[unit][:].rearrange("p e (u c) -> p u c e", u=2)
+            after_pair[unit] = work.tile([P, 2, 2 * P, 2], F32, name="after_pair")
+            for sign, op in enumerate((ALU.add, ALU.subtract)):
+                nc.vector.tensor_tensor(
+                    out=after_pair[unit][:, sign, :, :], in0=planes[:, 0, :, :], in1=planes[:, 1, :, :], op=op
+                )
+
+        def butterfly_half(unit):
+            planes = after_pair[unit][:].rearrange("p u (h k) e -> p h k u e", h=2)
+            grouped[unit] = work.tile([P, 2, P, 4], BF16, name="grouped", align_bytes=64)
+            for sign, op in enumerate((ALU.add, ALU.subtract)):
+                nc.vector.tensor_tensor(
+                    out=grouped[unit][:, sign, :, :].rearrange("p k (u e) -> p k u e", u=2),
+                    in0=planes[:, 0, :, :, :],
+                    in1=planes[:, 1, :, :, :],
+                    op=op,
+                )
+
+        def quantise(unit):
+            y_codes[unit] = ahead.tile([P, 2 * P], U32, name="y_codes", align_bytes=64)
+            y_scales[unit] = ahead.tile([P, 2 * P], U8, name="y_scales", align_bytes=64)
+            nc.vector.quantize_mx(
+                out=y_codes[unit][:].bitcast(FP8X4),
+                scales=y_scales[unit][:],
+                in_=grouped[unit][:].rearrange("p h k t -> p (h k t)"),
+            )
+
+        def multiply(unit):
+            tile_index, block = divmod(unit, BLOCKS)
+            if block == 0:
+                for n in range(N_TILES):
+                    acc[n] = acc_psum.tile([P, N_TILE], F32, name="acc%d" % n)
+            for half in range(2):
+                g = 2 * block + half
+                a, k = divmod(g, PLANES_PER_TILE)
+                tokens = slice(P * half, P * (half + 1))
+                for n in range(N_TILES):
+                    n_cols = slice(N_TILE * n, N_TILE * (n + 1))
+                    nc.tensor.matmul_mx(
+                        out=acc[n][:],
+                        lhsT=y_codes[unit][:, tokens].bitcast(FP8X4),
+                        lhsT_scale=y_scales[unit][:, tokens],
+                        rhs=w_words[g][:, n_cols].bitcast(FP8X4),
+                        rhs_scale=w_planes[4 * k : P, a, n_cols],
+                        start=(g == 0),
+                        stop=(g == GROUPS - 1),
+                    )
+            if block == BLOCKS - 1:
+                for n in range(N_TILES):
+                    result = store_pool.tile([P, N_TILE], F32, name="result")
+                    nc.scalar.copy(out=result[:], in_=acc[n][:])
+                    nc.sync.dma_start(
+                        out=out_rows[P * tile_index : P * (tile_index + 1), N_TILE * n : N_TILE * (n + 1)],
+                        in_=result[:],
+                    )
+
+        def in_range(unit):
+            return 0 <= unit < UNITS
+
+        for j in range(-3, UNITS + 1):
+            if in_range(j):
+                butterfly_odd(j)
+            if in_range(j - 1):
+                butterfly_half(j - 1)
+            if in_range(j):
+                butterfly_pair(j)
+            if in_range(j - 1):
+                quantise(j - 1)
+            if in_range(j + 2):
+                hadamard_over_partitions(j + 2)
+            if in_range(j + 3):
+                transpose_unit(j + 3)
+            if in_range(j - 1):
+                multiply(j - 1)

@@ -157,10 +157,12 @@ def tile_hadlinear_kernel(tc, x, weight_words, weight_scales, out):
         def butterfly_pair(unit):
             planes = after_odd[unit][:].rearrange("p e (u c) -> p u c e", u=2)
             after_pair[unit] = work.tile([P, 2, 2 * P, 2], F32, name="after_pair")
-            for sign, op in enumerate((ALU.add, ALU.subtract)):
-                nc.vector.tensor_tensor(
-                    out=after_pair[unit][:, sign, :, :], in0=planes[:, 0, :, :], in1=planes[:, 1, :, :], op=op
-                )
+            nc.vector.tensor_tensor(
+                out=after_pair[unit][:, 0, :, :], in0=planes[:, 0, :, :], in1=planes[:, 1, :, :], op=ALU.add
+            )
+            nc.gpsimd.tensor_tensor(
+                out=after_pair[unit][:, 1, :, :], in0=planes[:, 0, :, :], in1=planes[:, 1, :, :], op=ALU.subtract
+            )
 
         def butterfly_half(unit):
             planes = after_pair[unit][:].rearrange("p u (h k) e -> p h k u e", h=2)

@@ -25,6 +25,11 @@ UNITS = (TOKENS // P) * BLOCKS
 PLANES_PER_TILE = 4
 SCALE = 1.0 / 32.0
 
+SORT_AHEAD = 4
+TRANSPOSE_AHEAD = 3
+HADAMARD_AHEAD = 2
+MULTIPLY_BEHIND = 3
+
 FLOPS = 2 * TOKENS * FEATURES * OUTPUTS + 10 * TOKENS * FEATURES
 
 
@@ -38,11 +43,12 @@ def tile_hadlinear_kernel(tc, x, weight_words, weight_scales, out):
         x_pool = ctx.enter_context(tc.tile_pool(name="x_pool", bufs=UNITS))
         w_pool = ctx.enter_context(tc.tile_pool(name="w_pool", bufs=GROUPS))
         work = ctx.enter_context(tc.tile_pool(name="work", bufs=2))
-        ahead = ctx.enter_context(tc.tile_pool(name="ahead", bufs=3))
+        ahead = ctx.enter_context(tc.tile_pool(name="ahead", bufs=HADAMARD_AHEAD + 2))
+        behind = ctx.enter_context(tc.tile_pool(name="behind", bufs=MULTIPLY_BEHIND + 2))
         store_pool = ctx.enter_context(tc.tile_pool(name="store_pool", bufs=2 * N_TILES))
         t_psum = ctx.enter_context(tc.psum_pool(name="t_psum", bufs=1))
-        even_psum = ctx.enter_context(tc.psum_pool(name="even_psum", bufs=2))
-        odd_psum = ctx.enter_context(tc.psum_pool(name="odd_psum", bufs=1))
+        sum_psum = ctx.enter_context(tc.psum_pool(name="sum_psum", bufs=1))
+        odd_psum = ctx.enter_context(tc.psum_pool(name="odd_psum", bufs=2))
         acc_psum = ctx.enter_context(tc.psum_pool(name="acc_psum", bufs=1))
         ctx.enter_context(tc.manual_schedule())
 
@@ -110,9 +116,9 @@ def tile_hadlinear_kernel(tc, x, weight_words, weight_scales, out):
             out=hadamard[:], in0=bits[:], scalar1=-2.0, scalar2=1.0, op0=ALU.mult, op1=ALU.add
         )
 
+        x_sorted = {}
         x_t = {}
-        z_even = {}
-        z_odd_sb = {}
+        z_odd = {}
         after_odd = {}
         after_pair = {}
         grouped = {}
@@ -120,49 +126,47 @@ def tile_hadlinear_kernel(tc, x, weight_words, weight_scales, out):
         y_scales = {}
         acc = {}
 
+        def sort_words(unit):
+            x_sorted[unit] = work.tile([P, 4, P], F32, name="x_sorted")
+            nc.scalar.copy(
+                out=x_sorted[unit][:].rearrange("k (u h) p -> k u h p", u=2),
+                in_=x_chunk[unit][:].bitcast(F32).rearrange("k (h p u) -> k u h p", h=2, u=2),
+            )
+
         def transpose_unit(unit):
-            words = x_chunk[unit][:].bitcast(F32)
             t_bank = t_psum.tile([P, 4, P], F32, name="t_bank")
-            for pair in range(2):
-                for half in range(2):
-                    nc.tensor.transpose(
-                        t_bank[:, 2 * pair + half, :],
-                        words[:, 256 * half + pair : 256 * (half + 1) : 2],
-                        identity[:],
-                    )
-            x_t[unit] = ahead.tile([P, BLOCK], BF16, name="x_t")
+            for plane in range(4):
+                nc.tensor.transpose(t_bank[:, plane, :], x_sorted[unit][:, plane, :], identity[:])
+            x_t[unit] = work.tile([P, BLOCK], BF16, name="x_t")
             nc.scalar.copy(out=x_t[unit][:].bitcast(F32), in_=t_bank[:].rearrange("p s k -> p (s k)"))
 
         def hadamard_over_partitions(unit):
             columns = x_t[unit][:].rearrange("p (w e) -> p w e", e=2)
-            z_odd = odd_psum.tile([P, 4 * P], F32, name="z_odd")
-            z_even[unit] = even_psum.tile([P, 4 * P], F32, name="z_even")
-            nc.tensor.matmul(out=z_odd[:], lhsT=hadamard[:], rhs=columns[:, :, 1], start=True, stop=True)
-            nc.tensor.matmul(out=z_even[unit][:], lhsT=hadamard[:], rhs=columns[:, :, 0], start=True, stop=True)
-            z_odd_sb[unit] = ahead.tile([P, 4 * P], F32, name="z_odd_sb")
-            nc.scalar.mul(out=z_odd_sb[unit][:], in_=z_odd[:], mul=SCALE)
+            z_sum = sum_psum.tile([P, 4 * P], F32, name="z_sum")
+            z_odd[unit] = odd_psum.tile([P, 4 * P], F32, name="z_odd")
+            nc.tensor.matmul(out=z_sum[:], lhsT=hadamard[:], rhs=columns[:, :, 0], start=True, stop=False)
+            nc.tensor.matmul(out=z_sum[:], lhsT=hadamard[:], rhs=columns[:, :, 1], start=False, stop=True)
+            nc.tensor.matmul(out=z_odd[unit][:], lhsT=hadamard[:], rhs=columns[:, :, 1], start=True, stop=True)
+            after_odd[unit] = ahead.tile([P, 2, 4 * P], F32, name="after_odd")
+            nc.scalar.mul(out=after_odd[unit][:, 0, :], in_=z_sum[:], mul=SCALE)
 
-        def butterfly_odd(unit):
-            after_odd[unit] = work.tile([P, 2, 4 * P], F32, name="after_odd")
-            for sign, op in enumerate((ALU.add, ALU.subtract)):
-                nc.vector.scalar_tensor_tensor(
-                    out=after_odd[unit][:, sign, :],
-                    in0=z_even[unit][:],
-                    scalar=SCALE,
-                    in1=z_odd_sb[unit][:],
-                    op0=ALU.mult,
-                    op1=op,
-                )
+        def difference_odd(unit):
+            nc.vector.scalar_tensor_tensor(
+                out=after_odd[unit][:, 1, :],
+                in0=z_odd[unit][:],
+                scalar=-2.0 * SCALE,
+                in1=after_odd[unit][:, 0, :],
+                op0=ALU.mult,
+                op1=ALU.add,
+            )
 
         def butterfly_pair(unit):
             planes = after_odd[unit][:].rearrange("p e (u c) -> p u c e", u=2)
             after_pair[unit] = work.tile([P, 2, 2 * P, 2], F32, name="after_pair")
-            nc.vector.tensor_tensor(
-                out=after_pair[unit][:, 0, :, :], in0=planes[:, 0, :, :], in1=planes[:, 1, :, :], op=ALU.add
-            )
-            nc.gpsimd.tensor_tensor(
-                out=after_pair[unit][:, 1, :, :], in0=planes[:, 0, :, :], in1=planes[:, 1, :, :], op=ALU.subtract
-            )
+            for sign, op in enumerate((ALU.add, ALU.subtract)):
+                nc.vector.tensor_tensor(
+                    out=after_pair[unit][:, sign, :, :], in0=planes[:, 0, :, :], in1=planes[:, 1, :, :], op=op
+                )
 
         def butterfly_half(unit):
             planes = after_pair[unit][:].rearrange("p u (h k) e -> p h k u e", h=2)
@@ -176,8 +180,8 @@ def tile_hadlinear_kernel(tc, x, weight_words, weight_scales, out):
                 )
 
         def quantise(unit):
-            y_codes[unit] = ahead.tile([P, 2 * P], U32, name="y_codes", align_bytes=64)
-            y_scales[unit] = ahead.tile([P, 2 * P], U8, name="y_scales", align_bytes=64)
+            y_codes[unit] = behind.tile([P, 2 * P], U32, name="y_codes", align_bytes=64)
+            y_scales[unit] = behind.tile([P, 2 * P], U8, name="y_scales", align_bytes=64)
             nc.vector.quantize_mx(
                 out=y_codes[unit][:].bitcast(FP8X4),
                 scales=y_scales[unit][:],
@@ -186,15 +190,14 @@ def tile_hadlinear_kernel(tc, x, weight_words, weight_scales, out):
 
         def multiply(unit):
             tile_index, block = divmod(unit, BLOCKS)
-            if block == 0:
-                for n in range(N_TILES):
+            for n in range(N_TILES):
+                n_cols = slice(N_TILE * n, N_TILE * (n + 1))
+                if block == 0:
                     acc[n] = acc_psum.tile([P, N_TILE], F32, name="acc%d" % n)
-            for half in range(2):
-                g = 2 * block + half
-                a, k = divmod(g, PLANES_PER_TILE)
-                tokens = slice(P * half, P * (half + 1))
-                for n in range(N_TILES):
-                    n_cols = slice(N_TILE * n, N_TILE * (n + 1))
+                for half in range(2):
+                    g = 2 * block + half
+                    a, k = divmod(g, PLANES_PER_TILE)
+                    tokens = slice(P * half, P * (half + 1))
                     nc.tensor.matmul_mx(
                         out=acc[n][:],
                         lhsT=y_codes[unit][:, tokens].bitcast(FP8X4),
@@ -204,30 +207,28 @@ def tile_hadlinear_kernel(tc, x, weight_words, weight_scales, out):
                         start=(g == 0),
                         stop=(g == GROUPS - 1),
                     )
-            if block == BLOCKS - 1:
-                for n in range(N_TILES):
+                if block == BLOCKS - 1:
                     result = store_pool.tile([P, N_TILE], F32, name="result")
                     nc.scalar.copy(out=result[:], in_=acc[n][:])
-                    nc.sync.dma_start(
-                        out=out_rows[P * tile_index : P * (tile_index + 1), N_TILE * n : N_TILE * (n + 1)],
-                        in_=result[:],
-                    )
+                    nc.sync.dma_start(out=out_rows[P * tile_index : P * (tile_index + 1), n_cols], in_=result[:])
 
         def in_range(unit):
             return 0 <= unit < UNITS
 
-        for j in range(-3, UNITS + 1):
+        for j in range(-SORT_AHEAD, UNITS + MULTIPLY_BEHIND):
             if in_range(j):
-                butterfly_odd(j)
+                difference_odd(j)
             if in_range(j - 1):
                 butterfly_half(j - 1)
             if in_range(j):
                 butterfly_pair(j)
             if in_range(j - 1):
                 quantise(j - 1)
-            if in_range(j + 2):
-                hadamard_over_partitions(j + 2)
-            if in_range(j + 3):
-                transpose_unit(j + 3)
-            if in_range(j - 1):
-                multiply(j - 1)
+            if in_range(j + HADAMARD_AHEAD):
+                hadamard_over_partitions(j + HADAMARD_AHEAD)
+            if in_range(j + TRANSPOSE_AHEAD):
+                transpose_unit(j + TRANSPOSE_AHEAD)
+            if in_range(j + SORT_AHEAD):
+                sort_words(j + SORT_AHEAD)
+            if in_range(j - MULTIPLY_BEHIND):
+                multiply(j - MULTIPLY_BEHIND)

@@ -28,7 +28,9 @@ SCALE = 1.0 / 32.0
 SORT_AHEAD = 4
 TRANSPOSE_AHEAD = 3
 HADAMARD_AHEAD = 2
-MULTIPLY_BEHIND = 3
+SIDES = 2
+LEFT_BEHIND = 1
+RIGHT_BEHIND = LEFT_BEHIND + 3
 
 FLOPS = 2 * TOKENS * FEATURES * OUTPUTS + 10 * TOKENS * FEATURES
 
@@ -41,10 +43,10 @@ def tile_hadlinear_kernel(tc, x, weight_words, weight_scales, out):
     with ExitStack() as ctx:
         const = ctx.enter_context(tc.tile_pool(name="const", bufs=1))
         x_pool = ctx.enter_context(tc.tile_pool(name="x_pool", bufs=UNITS))
-        w_pool = ctx.enter_context(tc.tile_pool(name="w_pool", bufs=GROUPS))
+        w_pool = ctx.enter_context(tc.tile_pool(name="w_pool", bufs=SIDES * GROUPS))
         work = ctx.enter_context(tc.tile_pool(name="work", bufs=2))
         ahead = ctx.enter_context(tc.tile_pool(name="ahead", bufs=HADAMARD_AHEAD + 2))
-        behind = ctx.enter_context(tc.tile_pool(name="behind", bufs=MULTIPLY_BEHIND + 2))
+        behind = ctx.enter_context(tc.tile_pool(name="behind", bufs=RIGHT_BEHIND + 2))
         store_pool = ctx.enter_context(tc.tile_pool(name="store_pool", bufs=2 * N_TILES))
         t_psum = ctx.enter_context(tc.psum_pool(name="t_psum", bufs=1))
         sum_psum = ctx.enter_context(tc.psum_pool(name="sum_psum", bufs=1))
@@ -63,11 +65,14 @@ def tile_hadlinear_kernel(tc, x, weight_words, weight_scales, out):
                 in_=x_rows[P * tile_index : P * (tile_index + 1), BLOCK * block : BLOCK * (block + 1)],
             )
 
-        def load_w(g):
-            w_words[g] = w_pool.tile([P, OUTPUTS], U32, name="w_words", align_bytes=64)
+        def load_w(g, side):
+            w_words[(g, side)] = w_pool.tile([P, OUTPUTS // SIDES], U32, name="w_words", align_bytes=64)
+            side_bytes = 4 * OUTPUTS // SIDES
             nc.sync.dma_start(
-                out=w_words[g][:].bitcast(I32),
-                in_=weight_words[g].rearrange("p n t -> p (n t)").bitcast(I32),
+                out=w_words[(g, side)][:].bitcast(I32),
+                in_=weight_words[g]
+                .rearrange("p n t -> p (n t)")[:, side_bytes * side : side_bytes * (side + 1)]
+                .bitcast(I32),
             )
 
         w_planes = const.tile([P, GROUPS // PLANES_PER_TILE, OUTPUTS], U8, align_bytes=64)
@@ -83,10 +88,12 @@ def tile_hadlinear_kernel(tc, x, weight_words, weight_scales, out):
                         PLANES_PER_TILE * a : PLANES_PER_TILE * (a + 1), 4 * quadrant : 4 * quadrant + 4, :
                     ].bitcast(I32),
                 )
-        for g in range(GROUPS):
-            load_w(g)
-            load_x(BLOCKS + g)
-        for unit in range(BLOCKS + GROUPS, UNITS):
+        for side in range(SIDES):
+            for block in range(BLOCKS):
+                load_w(2 * block, side)
+                load_w(2 * block + 1, side)
+                load_x(BLOCKS * (side + 1) + block)
+        for unit in range(BLOCKS * (SIDES + 1), UNITS):
             load_x(unit)
 
         warm = const.tile([P, 1], F32)
@@ -140,15 +147,18 @@ def tile_hadlinear_kernel(tc, x, weight_words, weight_scales, out):
             x_t[unit] = work.tile([P, BLOCK], BF16, name="x_t")
             nc.scalar.copy(out=x_t[unit][:].bitcast(F32), in_=t_bank[:].rearrange("p s k -> p (s k)"))
 
-        def hadamard_over_partitions(unit):
+        def hadamard_sum(unit):
             columns = x_t[unit][:].rearrange("p (w e) -> p w e", e=2)
             z_sum = sum_psum.tile([P, 4 * P], F32, name="z_sum")
-            z_odd[unit] = odd_psum.tile([P, 4 * P], F32, name="z_odd")
             nc.tensor.matmul(out=z_sum[:], lhsT=hadamard[:], rhs=columns[:, :, 0], start=True, stop=False)
             nc.tensor.matmul(out=z_sum[:], lhsT=hadamard[:], rhs=columns[:, :, 1], start=False, stop=True)
-            nc.tensor.matmul(out=z_odd[unit][:], lhsT=hadamard[:], rhs=columns[:, :, 1], start=True, stop=True)
             after_odd[unit] = ahead.tile([P, 2, 4 * P], F32, name="after_odd")
             nc.scalar.mul(out=after_odd[unit][:, 0, :], in_=z_sum[:], mul=SCALE)
+
+        def hadamard_odd(unit):
+            columns = x_t[unit][:].rearrange("p (w e) -> p w e", e=2)
+            z_odd[unit] = odd_psum.tile([P, 4 * P], F32, name="z_odd")
+            nc.tensor.matmul(out=z_odd[unit][:], lhsT=hadamard[:], rhs=columns[:, :, 1], start=True, stop=True)
 
         def difference_odd(unit):
             nc.vector.scalar_tensor_tensor(
@@ -188,10 +198,12 @@ def tile_hadlinear_kernel(tc, x, weight_words, weight_scales, out):
                 in_=grouped[unit][:].rearrange("p h k t -> p (h k t)"),
             )
 
-        def multiply(unit):
+        def multiply(unit, side):
             tile_index, block = divmod(unit, BLOCKS)
-            for n in range(N_TILES):
+            tiles_per_side = N_TILES // SIDES
+            for n in range(tiles_per_side * side, tiles_per_side * (side + 1)):
                 n_cols = slice(N_TILE * n, N_TILE * (n + 1))
+                side_cols = slice(N_TILE * (n % tiles_per_side), N_TILE * (n % tiles_per_side + 1))
                 if block == 0:
                     acc[n] = acc_psum.tile([P, N_TILE], F32, name="acc%d" % n)
                 for half in range(2):
@@ -202,7 +214,7 @@ def tile_hadlinear_kernel(tc, x, weight_words, weight_scales, out):
                         out=acc[n][:],
                         lhsT=y_codes[unit][:, tokens].bitcast(FP8X4),
                         lhsT_scale=y_scales[unit][:, tokens],
-                        rhs=w_words[g][:, n_cols].bitcast(FP8X4),
+                        rhs=w_words[(g, side)][:, side_cols].bitcast(FP8X4),
                         rhs_scale=w_planes[4 * k : P, a, n_cols],
                         start=(g == 0),
                         stop=(g == GROUPS - 1),
@@ -215,7 +227,7 @@ def tile_hadlinear_kernel(tc, x, weight_words, weight_scales, out):
         def in_range(unit):
             return 0 <= unit < UNITS
 
-        for j in range(-SORT_AHEAD, UNITS + MULTIPLY_BEHIND):
+        for j in range(-SORT_AHEAD, UNITS + RIGHT_BEHIND):
             if in_range(j):
                 difference_odd(j)
             if in_range(j - 1):
@@ -225,10 +237,14 @@ def tile_hadlinear_kernel(tc, x, weight_words, weight_scales, out):
             if in_range(j - 1):
                 quantise(j - 1)
             if in_range(j + HADAMARD_AHEAD):
-                hadamard_over_partitions(j + HADAMARD_AHEAD)
+                hadamard_sum(j + HADAMARD_AHEAD)
             if in_range(j + TRANSPOSE_AHEAD):
                 transpose_unit(j + TRANSPOSE_AHEAD)
+            if in_range(j + HADAMARD_AHEAD):
+                hadamard_odd(j + HADAMARD_AHEAD)
             if in_range(j + SORT_AHEAD):
                 sort_words(j + SORT_AHEAD)
-            if in_range(j - MULTIPLY_BEHIND):
-                multiply(j - MULTIPLY_BEHIND)
+            if in_range(j - LEFT_BEHIND):
+                multiply(j - LEFT_BEHIND, 0)
+            if in_range(j - RIGHT_BEHIND):
+                multiply(j - RIGHT_BEHIND, 1)

@@ -238,10 +238,9 @@ def tile_hadlinear_kernel(tc, x, weight_words, weight_scales, out):
                 quantise(j - 1)
             if in_range(j + HADAMARD_AHEAD):
                 hadamard_sum(j + HADAMARD_AHEAD)
+                hadamard_odd(j + HADAMARD_AHEAD)
             if in_range(j + TRANSPOSE_AHEAD):
                 transpose_unit(j + TRANSPOSE_AHEAD)
-            if in_range(j + HADAMARD_AHEAD):
-                hadamard_odd(j + HADAMARD_AHEAD)
             if in_range(j + SORT_AHEAD):
                 sort_words(j + SORT_AHEAD)
             if in_range(j - LEFT_BEHIND):

@@ -25,7 +25,6 @@ UNITS = (TOKENS // P) * BLOCKS
 PLANES_PER_TILE = 4
 SCALE = 1.0 / 32.0
 
-SORT_AHEAD = 4
 TRANSPOSE_AHEAD = 3
 HADAMARD_AHEAD = 2
 SIDES = 2
@@ -123,7 +122,6 @@ def tile_hadlinear_kernel(tc, x, weight_words, weight_scales, out):
             out=hadamard[:], in0=bits[:], scalar1=-2.0, scalar2=1.0, op0=ALU.mult, op1=ALU.add
         )
 
-        x_sorted = {}
         x_t = {}
         z_odd = {}
         after_odd = {}
@@ -133,17 +131,16 @@ def tile_hadlinear_kernel(tc, x, weight_words, weight_scales, out):
         y_scales = {}
         acc = {}
 
-        def sort_words(unit):
-            x_sorted[unit] = work.tile([P, 4, P], F32, name="x_sorted")
-            nc.scalar.copy(
-                out=x_sorted[unit][:].rearrange("k (u h) p -> k u h p", u=2),
-                in_=x_chunk[unit][:].bitcast(F32).rearrange("k (h p u) -> k u h p", h=2, u=2),
-            )
-
         def transpose_unit(unit):
+            words = x_chunk[unit][:].bitcast(F32)
             t_bank = t_psum.tile([P, 4, P], F32, name="t_bank")
-            for plane in range(4):
-                nc.tensor.transpose(t_bank[:, plane, :], x_sorted[unit][:, plane, :], identity[:])
+            for pair in range(2):
+                for half in range(2):
+                    nc.tensor.transpose(
+                        t_bank[:, 2 * pair + half, :],
+                        words[:, 256 * half + pair : 256 * (half + 1) : 2],
+                        identity[:],
+                    )
             x_t[unit] = work.tile([P, BLOCK], BF16, name="x_t")
             nc.scalar.copy(out=x_t[unit][:].bitcast(F32), in_=t_bank[:].rearrange("p s k -> p (s k)"))
 
@@ -227,7 +224,7 @@ def tile_hadlinear_kernel(tc, x, weight_words, weight_scales, out):
         def in_range(unit):
             return 0 <= unit < UNITS
 
-        for j in range(-SORT_AHEAD, UNITS + RIGHT_BEHIND):
+        for j in range(-TRANSPOSE_AHEAD, UNITS + RIGHT_BEHIND):
             if in_range(j):
                 difference_odd(j)
             if in_range(j - 1):
@@ -241,8 +238,6 @@ def tile_hadlinear_kernel(tc, x, weight_words, weight_scales, out):
                 hadamard_odd(j + HADAMARD_AHEAD)
             if in_range(j + TRANSPOSE_AHEAD):
                 transpose_unit(j + TRANSPOSE_AHEAD)
-            if in_range(j + SORT_AHEAD):
-                sort_words(j + SORT_AHEAD)
             if in_range(j - LEFT_BEHIND):
                 multiply(j - LEFT_BEHIND, 0)
             if in_range(j - RIGHT_BEHIND):

@@ -25,11 +25,13 @@ UNITS = (TOKENS // P) * BLOCKS
 PLANES_PER_TILE = 4
 SCALE = 1.0 / 32.0
 
-TRANSPOSE_AHEAD = 3
 HADAMARD_AHEAD = 2
-SIDES = 2
+TRANSPOSE_AHEAD = 3
+FIRST_STEP = -3
+TENSOR_SUMS = 10
 LEFT_BEHIND = 1
-RIGHT_BEHIND = LEFT_BEHIND + 3
+RIGHT_LAG = [max(0, 4 - (u + 1) // BLOCKS) for u in range(UNITS)]
+SIDES = 2
 
 FLOPS = 2 * TOKENS * FEATURES * OUTPUTS + 10 * TOKENS * FEATURES
 
@@ -41,11 +43,12 @@ def tile_hadlinear_kernel(tc, x, weight_words, weight_scales, out):
 
     with ExitStack() as ctx:
         const = ctx.enter_context(tc.tile_pool(name="const", bufs=1))
+        xt_pool = ctx.enter_context(tc.tile_pool(name="xt_pool", bufs=4))
         x_pool = ctx.enter_context(tc.tile_pool(name="x_pool", bufs=UNITS))
         w_pool = ctx.enter_context(tc.tile_pool(name="w_pool", bufs=SIDES * GROUPS))
         work = ctx.enter_context(tc.tile_pool(name="work", bufs=2))
         ahead = ctx.enter_context(tc.tile_pool(name="ahead", bufs=HADAMARD_AHEAD + 2))
-        behind = ctx.enter_context(tc.tile_pool(name="behind", bufs=RIGHT_BEHIND + 2))
+        behind = ctx.enter_context(tc.tile_pool(name="behind", bufs=8))
         store_pool = ctx.enter_context(tc.tile_pool(name="store_pool", bufs=2 * N_TILES))
         t_psum = ctx.enter_context(tc.psum_pool(name="t_psum", bufs=1))
         sum_psum = ctx.enter_context(tc.psum_pool(name="sum_psum", bufs=1))
@@ -77,9 +80,7 @@ def tile_hadlinear_kernel(tc, x, weight_words, weight_scales, out):
         w_planes = const.tile([P, GROUPS // PLANES_PER_TILE, OUTPUTS], U8, align_bytes=64)
         nc.vector.memset(w_planes[:].rearrange("p a n -> p (a n)").bitcast(I32), 0)
 
-        for unit in range(BLOCKS):
-            load_x(unit)
-        for a in range(GROUPS // PLANES_PER_TILE):
+        def load_scales(a):
             for quadrant in range(4):
                 nc.sync.dma_start(
                     out=w_planes[32 * quadrant : 32 * quadrant + 16, a, :].bitcast(I32),
@@ -87,12 +88,22 @@ def tile_hadlinear_kernel(tc, x, weight_words, weight_scales, out):
                         PLANES_PER_TILE * a : PLANES_PER_TILE * (a + 1), 4 * quadrant : 4 * quadrant + 4, :
                     ].bitcast(I32),
                 )
+        for unit in range(BLOCKS):
+            load_x(unit)
+        load_scales(0)
+        load_w(0, 0)
+        load_w(1, 0)
+        load_scales(1)
+        next_x = BLOCKS
         for side in range(SIDES):
             for block in range(BLOCKS):
-                load_w(2 * block, side)
-                load_w(2 * block + 1, side)
-                load_x(BLOCKS * (side + 1) + block)
-        for unit in range(BLOCKS * (SIDES + 1), UNITS):
+                if side > 0 or block > 0:
+                    load_w(2 * block, side)
+                    load_w(2 * block + 1, side)
+                for unit in range(next_x, next_x + (2 if (side, block) == (0, 1) else 1)):
+                    load_x(unit)
+                    next_x = unit + 1
+        for unit in range(next_x, UNITS):
             load_x(unit)
 
         warm = const.tile([P, 1], F32)
@@ -124,12 +135,49 @@ def tile_hadlinear_kernel(tc, x, weight_words, weight_scales, out):
 
         x_t = {}
         z_odd = {}
+        z_even = {}
         after_odd = {}
         after_pair = {}
         grouped = {}
         y_codes = {}
         y_scales = {}
         acc = {}
+
+        def first_bank(name, n):
+            return acc_psum.tile([P, N_TILE], F32, name=name, tag="acc%d" % n)
+
+        def start_first_unit():
+            words = x_chunk[0][:].bitcast(F32)
+            x_t[0] = xt_pool.tile([P, BLOCK], BF16, name="x_t")
+            after_odd[0] = ahead.tile([P, 2, 4 * P], F32, name="after_odd")
+            banks = [first_bank("first_t", 2 * pair) for pair in range(2)]
+            for pair in range(2):
+                for half in range(2):
+                    nc.tensor.transpose(
+                        banks[pair][:, P * half : P * (half + 1)],
+                        words[:, 256 * half + pair : 256 * (half + 1) : 2],
+                        identity[:],
+                    )
+                nc.scalar.copy(
+                    out=x_t[0][:, 4 * P * pair : 4 * P * (pair + 1)].bitcast(F32), in_=banks[pair][:, 0 : 2 * P]
+                )
+            for pair in range(2):
+                cols = slice(2 * P * pair, 2 * P * (pair + 1))
+                z_sum = first_bank("first_sum", 2 * pair + 1)
+                z_first = odd_psum.tile([P, 4 * P], F32, name="z_odd")
+                columns = x_t[0][:, 4 * P * pair : 4 * P * (pair + 1)].rearrange("p (w e) -> p w e", e=2)
+                nc.tensor.matmul(out=z_sum[:, 0 : 2 * P], lhsT=hadamard[:], rhs=columns[:, :, 0], start=True, stop=False)
+                nc.tensor.matmul(out=z_sum[:, 0 : 2 * P], lhsT=hadamard[:], rhs=columns[:, :, 1], start=False, stop=True)
+                nc.scalar.mul(out=after_odd[0][:, 0, cols], in_=z_sum[:, 0 : 2 * P], mul=SCALE)
+                nc.tensor.matmul(out=z_first[:, 0 : 2 * P], lhsT=hadamard[:], rhs=columns[:, :, 1], start=True, stop=True)
+                nc.vector.scalar_tensor_tensor(
+                    out=after_odd[0][:, 1, cols],
+                    in0=z_first[:, 0 : 2 * P],
+                    scalar=-2.0 * SCALE,
+                    in1=after_odd[0][:, 0, cols],
+                    op0=ALU.mult,
+                    op1=ALU.add,
+                )
 
         def transpose_unit(unit):
             words = x_chunk[unit][:].bitcast(F32)
@@ -141,16 +189,22 @@ def tile_hadlinear_kernel(tc, x, weight_words, weight_scales, out):
                         words[:, 256 * half + pair : 256 * (half + 1) : 2],
                         identity[:],
                     )
-            x_t[unit] = work.tile([P, BLOCK], BF16, name="x_t")
+            x_t[unit] = xt_pool.tile([P, BLOCK], BF16, name="x_t")
             nc.scalar.copy(out=x_t[unit][:].bitcast(F32), in_=t_bank[:].rearrange("p s k -> p (s k)"))
 
         def hadamard_sum(unit):
             columns = x_t[unit][:].rearrange("p (w e) -> p w e", e=2)
             z_sum = sum_psum.tile([P, 4 * P], F32, name="z_sum")
-            nc.tensor.matmul(out=z_sum[:], lhsT=hadamard[:], rhs=columns[:, :, 0], start=True, stop=False)
-            nc.tensor.matmul(out=z_sum[:], lhsT=hadamard[:], rhs=columns[:, :, 1], start=False, stop=True)
+            on_tensor = unit < TENSOR_SUMS
+            nc.tensor.matmul(out=z_sum[:], lhsT=hadamard[:], rhs=columns[:, :, 0], start=True, stop=not on_tensor)
+            if on_tensor:
+                nc.tensor.matmul(out=z_sum[:], lhsT=hadamard[:], rhs=columns[:, :, 1], start=False, stop=True)
             after_odd[unit] = ahead.tile([P, 2, 4 * P], F32, name="after_odd")
-            nc.scalar.mul(out=after_odd[unit][:, 0, :], in_=z_sum[:], mul=SCALE)
+            if on_tensor:
+                nc.scalar.mul(out=after_odd[unit][:, 0, :], in_=z_sum[:], mul=SCALE)
+            else:
+                z_even[unit] = ahead.tile([P, 4 * P], F32, name="z_even")
+                nc.scalar.mul(out=z_even[unit][:], in_=z_sum[:], mul=SCALE)
 
         def hadamard_odd(unit):
             columns = x_t[unit][:].rearrange("p (w e) -> p w e", e=2)
@@ -158,6 +212,17 @@ def tile_hadlinear_kernel(tc, x, weight_words, weight_scales, out):
             nc.tensor.matmul(out=z_odd[unit][:], lhsT=hadamard[:], rhs=columns[:, :, 1], start=True, stop=True)
 
         def difference_odd(unit):
+            if unit >= TENSOR_SUMS:
+                for sign, scalar in enumerate((SCALE, -SCALE)):
+                    nc.vector.scalar_tensor_tensor(
+                        out=after_odd[unit][:, sign, :],
+                        in0=z_odd[unit][:],
+                        scalar=scalar,
+                        in1=z_even[unit][:],
+                        op0=ALU.mult,
+                        op1=ALU.add,
+                    )
+                return
             nc.vector.scalar_tensor_tensor(
                 out=after_odd[unit][:, 1, :],
                 in0=z_odd[unit][:],
@@ -224,21 +289,31 @@ def tile_hadlinear_kernel(tc, x, weight_words, weight_scales, out):
         def in_range(unit):
             return 0 <= unit < UNITS
 
-        for j in range(-TRANSPOSE_AHEAD, UNITS + RIGHT_BEHIND):
-            if in_range(j):
+        for j in range(FIRST_STEP, UNITS + LEFT_BEHIND):
+            if j == FIRST_STEP:
+                start_first_unit()
+            if in_range(j) and j > 0:
                 difference_odd(j)
-            if in_range(j - 1):
+            if in_range(j - 1) and j > 1:
                 butterfly_half(j - 1)
             if in_range(j):
                 butterfly_pair(j)
-            if in_range(j - 1):
+            if j == 0:
+                butterfly_half(0)
+                quantise(0)
+            if in_range(j - 1) and j > 1:
                 quantise(j - 1)
-            if in_range(j + HADAMARD_AHEAD):
+            if in_range(j + HADAMARD_AHEAD) and j + HADAMARD_AHEAD > 0:
                 hadamard_sum(j + HADAMARD_AHEAD)
                 hadamard_odd(j + HADAMARD_AHEAD)
-            if in_range(j + TRANSPOSE_AHEAD):
+            if in_range(j + TRANSPOSE_AHEAD) and j + TRANSPOSE_AHEAD > 1:
                 transpose_unit(j + TRANSPOSE_AHEAD)
-            if in_range(j - LEFT_BEHIND):
+            if j == FIRST_STEP:
+                transpose_unit(1)
+            if j == 0:
+                multiply(0, 0)
+            if in_range(j - LEFT_BEHIND) and j > LEFT_BEHIND:
                 multiply(j - LEFT_BEHIND, 0)
-            if in_range(j - RIGHT_BEHIND):
-                multiply(j - RIGHT_BEHIND, 1)
+            for unit in range(UNITS):
+                if unit + LEFT_BEHIND + RIGHT_LAG[unit] == j:
+                    multiply(unit, 1)

@@ -26,11 +26,11 @@ PLANES_PER_TILE = 4
 SCALE = 1.0 / 32.0
 
 HADAMARD_AHEAD = 2
-TRANSPOSE_AHEAD = 3
+TRANSPOSE_AHEAD = [4 if u <= BLOCKS else 3 for u in range(UNITS)]
 FIRST_STEP = -3
-TENSOR_SUMS = 10
+PLAIN_MATMULS = [3] + [4] * 3 + [3] * 4 + [2] * 4 + [3] * 4
 LEFT_BEHIND = 1
-RIGHT_LAG = [max(0, 4 - (u + 1) // BLOCKS) for u in range(UNITS)]
+RIGHT_LAG = [max(1, min(3, 3 - (u - 3) // BLOCKS)) for u in range(UNITS)]
 SIDES = 2
 
 FLOPS = 2 * TOKENS * FEATURES * OUTPUTS + 10 * TOKENS * FEATURES
@@ -94,16 +94,13 @@ def tile_hadlinear_kernel(tc, x, weight_words, weight_scales, out):
         load_w(0, 0)
         load_w(1, 0)
         load_scales(1)
-        next_x = BLOCKS
         for side in range(SIDES):
             for block in range(BLOCKS):
                 if side > 0 or block > 0:
                     load_w(2 * block, side)
                     load_w(2 * block + 1, side)
-                for unit in range(next_x, next_x + (2 if (side, block) == (0, 1) else 1)):
-                    load_x(unit)
-                    next_x = unit + 1
-        for unit in range(next_x, UNITS):
+                load_x(BLOCKS * (side + 1) + block)
+        for unit in range(BLOCKS * (SIDES + 1), UNITS):
             load_x(unit)
 
         warm = const.tile([P, 1], F32)
@@ -131,6 +128,10 @@ def tile_hadlinear_kernel(tc, x, weight_words, weight_scales, out):
         hadamard = const.tile([P, P], BF16)
         nc.vector.tensor_scalar(
             out=hadamard[:], in0=bits[:], scalar1=-2.0, scalar2=1.0, op0=ALU.mult, op1=ALU.add
+        )
+        minus_hadamard = const.tile([P, P], BF16)
+        nc.vector.tensor_scalar(
+            out=minus_hadamard[:], in0=bits[:], scalar1=2.0, scalar2=-1.0, op0=ALU.mult, op1=ALU.add
         )
 
         x_t = {}
@@ -169,15 +170,9 @@ def tile_hadlinear_kernel(tc, x, weight_words, weight_scales, out):
                 nc.tensor.matmul(out=z_sum[:, 0 : 2 * P], lhsT=hadamard[:], rhs=columns[:, :, 0], start=True, stop=False)
                 nc.tensor.matmul(out=z_sum[:, 0 : 2 * P], lhsT=hadamard[:], rhs=columns[:, :, 1], start=False, stop=True)
                 nc.scalar.mul(out=after_odd[0][:, 0, cols], in_=z_sum[:, 0 : 2 * P], mul=SCALE)
-                nc.tensor.matmul(out=z_first[:, 0 : 2 * P], lhsT=hadamard[:], rhs=columns[:, :, 1], start=True, stop=True)
-                nc.vector.scalar_tensor_tensor(
-                    out=after_odd[0][:, 1, cols],
-                    in0=z_first[:, 0 : 2 * P],
-                    scalar=-2.0 * SCALE,
-                    in1=after_odd[0][:, 0, cols],
-                    op0=ALU.mult,
-                    op1=ALU.add,
-                )
+                nc.tensor.matmul(out=z_first[:, 0 : 2 * P], lhsT=hadamard[:], rhs=columns[:, :, 0], start=True, stop=False)
+                nc.tensor.matmul(out=z_first[:, 0 : 2 * P], lhsT=minus_hadamard[:], rhs=columns[:, :, 1], start=False, stop=True)
+                nc.vector.tensor_single_scalar(out=after_odd[0][:, 1, cols], in_=z_first[:, 0 : 2 * P], scalar=SCALE, op=ALU.mult)
 
         def transpose_unit(unit):
             words = x_chunk[unit][:].bitcast(F32)
@@ -195,7 +190,7 @@ def tile_hadlinear_kernel(tc, x, weight_words, weight_scales, out):
         def hadamard_sum(unit):
             columns = x_t[unit][:].rearrange("p (w e) -> p w e", e=2)
             z_sum = sum_psum.tile([P, 4 * P], F32, name="z_sum")
-            on_tensor = unit < TENSOR_SUMS
+            on_tensor = PLAIN_MATMULS[unit] >= 3
             nc.tensor.matmul(out=z_sum[:], lhsT=hadamard[:], rhs=columns[:, :, 0], start=True, stop=not on_tensor)
             if on_tensor:
                 nc.tensor.matmul(out=z_sum[:], lhsT=hadamard[:], rhs=columns[:, :, 1], start=False, stop=True)
@@ -209,10 +204,17 @@ def tile_hadlinear_kernel(tc, x, weight_words, weight_scales, out):
         def hadamard_odd(unit):
             columns = x_t[unit][:].rearrange("p (w e) -> p w e", e=2)
             z_odd[unit] = odd_psum.tile([P, 4 * P], F32, name="z_odd")
-            nc.tensor.matmul(out=z_odd[unit][:], lhsT=hadamard[:], rhs=columns[:, :, 1], start=True, stop=True)
+            if PLAIN_MATMULS[unit] == 4:
+                nc.tensor.matmul(out=z_odd[unit][:], lhsT=hadamard[:], rhs=columns[:, :, 0], start=True, stop=False)
+                nc.tensor.matmul(out=z_odd[unit][:], lhsT=minus_hadamard[:], rhs=columns[:, :, 1], start=False, stop=True)
+                nc.scalar.mul(out=after_odd[unit][:, 1, :], in_=z_odd[unit][:], mul=SCALE)
+            else:
+                nc.tensor.matmul(out=z_odd[unit][:], lhsT=hadamard[:], rhs=columns[:, :, 1], start=True, stop=True)
 
         def difference_odd(unit):
-            if unit >= TENSOR_SUMS:
+            if PLAIN_MATMULS[unit] == 4:
+                return
+            if PLAIN_MATMULS[unit] == 2:
                 for sign, scalar in enumerate((SCALE, -SCALE)):
                     nc.vector.scalar_tensor_tensor(
                         out=after_odd[unit][:, sign, :],
@@ -289,7 +291,7 @@ def tile_hadlinear_kernel(tc, x, weight_words, weight_scales, out):
         def in_range(unit):
             return 0 <= unit < UNITS
 
-        for j in range(FIRST_STEP, UNITS + LEFT_BEHIND):
+        for j in range(FIRST_STEP, UNITS + LEFT_BEHIND + RIGHT_LAG[-1]):
             if j == FIRST_STEP:
                 start_first_unit()
             if in_range(j) and j > 0:
@@ -306,10 +308,9 @@ def tile_hadlinear_kernel(tc, x, weight_words, weight_scales, out):
             if in_range(j + HADAMARD_AHEAD) and j + HADAMARD_AHEAD > 0:
                 hadamard_sum(j + HADAMARD_AHEAD)
                 hadamard_odd(j + HADAMARD_AHEAD)
-            if in_range(j + TRANSPOSE_AHEAD) and j + TRANSPOSE_AHEAD > 1:
-                transpose_unit(j + TRANSPOSE_AHEAD)
-            if j == FIRST_STEP:
-                transpose_unit(1)
+            for unit in range(1, UNITS):
+                if unit - TRANSPOSE_AHEAD[unit] == j:
+                    transpose_unit(unit)
             if j == 0:
                 multiply(0, 0)
             if in_range(j - LEFT_BEHIND) and j > LEFT_BEHIND:

@@ -26,11 +26,14 @@ PLANES_PER_TILE = 4
 SCALE = 1.0 / 32.0
 
 HADAMARD_AHEAD = 2
-TRANSPOSE_AHEAD = [4 if u <= BLOCKS else 3 for u in range(UNITS)]
+X_AHEAD_OF_W = BLOCKS + 1
+TRANSPOSE_AHEAD = [4 if u < X_AHEAD_OF_W else 3 for u in range(UNITS)]
 FIRST_STEP = -3
-PLAIN_MATMULS = [3] + [4] * 3 + [3] * 4 + [2] * 4 + [3] * 4
+PLAIN_MATMULS = [4] * 7 + [2] * 5 + [3] * 4
 LEFT_BEHIND = 1
-RIGHT_LAG = [max(1, min(3, 3 - (u - 3) // BLOCKS)) for u in range(UNITS)]
+RIGHT_LAG = [max(2, min(4, 4 - (u - 3) // BLOCKS)) for u in range(UNITS)]
+W_LANDED = 2 * BLOCKS
+WARM_UP = 4
 SIDES = 2
 
 FLOPS = 2 * TOKENS * FEATURES * OUTPUTS + 10 * TOKENS * FEATURES
@@ -50,8 +53,7 @@ def tile_hadlinear_kernel(tc, x, weight_words, weight_scales, out):
         ahead = ctx.enter_context(tc.tile_pool(name="ahead", bufs=HADAMARD_AHEAD + 2))
         behind = ctx.enter_context(tc.tile_pool(name="behind", bufs=8))
         store_pool = ctx.enter_context(tc.tile_pool(name="store_pool", bufs=2 * N_TILES))
-        t_psum = ctx.enter_context(tc.psum_pool(name="t_psum", bufs=1))
-        sum_psum = ctx.enter_context(tc.psum_pool(name="sum_psum", bufs=1))
+        turn_psum = ctx.enter_context(tc.psum_pool(name="turn_psum", bufs=2))
         odd_psum = ctx.enter_context(tc.psum_pool(name="odd_psum", bufs=2))
         acc_psum = ctx.enter_context(tc.psum_pool(name="acc_psum", bufs=1))
         ctx.enter_context(tc.manual_schedule())
@@ -88,19 +90,17 @@ def tile_hadlinear_kernel(tc, x, weight_words, weight_scales, out):
                         PLANES_PER_TILE * a : PLANES_PER_TILE * (a + 1), 4 * quadrant : 4 * quadrant + 4, :
                     ].bitcast(I32),
                 )
-        for unit in range(BLOCKS):
+        for unit in range(X_AHEAD_OF_W):
             load_x(unit)
         load_scales(0)
-        load_w(0, 0)
-        load_w(1, 0)
-        load_scales(1)
         for side in range(SIDES):
             for block in range(BLOCKS):
-                if side > 0 or block > 0:
-                    load_w(2 * block, side)
-                    load_w(2 * block + 1, side)
-                load_x(BLOCKS * (side + 1) + block)
-        for unit in range(BLOCKS * (SIDES + 1), UNITS):
+                load_w(2 * block, side)
+                load_w(2 * block + 1, side)
+                if side == 0 and block == 1:
+                    load_scales(1)
+                load_x(X_AHEAD_OF_W + BLOCKS * side + block)
+        for unit in range(X_AHEAD_OF_W + BLOCKS * SIDES, UNITS):
             load_x(unit)
 
         warm = const.tile([P, 1], F32)
@@ -111,6 +111,11 @@ def tile_hadlinear_kernel(tc, x, weight_words, weight_scales, out):
         col_index = const.tile([P, P], I32)
         nc.gpsimd.iota(row_index[:], pattern=[[0, P]], base=0, channel_multiplier=1)
         nc.gpsimd.iota(col_index[:], pattern=[[1, P]], base=0, channel_multiplier=0)
+        zeros = const.tile([P, P], F32)
+        nc.gpsimd.memset(zeros[:], 0.0)
+        warm_bank = acc_psum.tile([P, N_TILE], F32, name="warm_bank", tag="acc3")
+        for _ in range(WARM_UP):
+            nc.tensor.matmul(out=warm_bank[:, 0:P], lhsT=zeros[:], rhs=zeros[:], start=True, stop=True)
         identity = const.tile([P, P], F32)
         masks.make_identity(nc, identity[:])
         bits = const.tile([P, P], I32)
@@ -143,6 +148,10 @@ def tile_hadlinear_kernel(tc, x, weight_words, weight_scales, out):
         y_codes = {}
         y_scales = {}
         acc = {}
+        tiles_per_side = N_TILES // SIDES
+
+        def bank_in_turn(name):
+            return turn_psum.tile([P, 4 * P], F32, name=name, tag="turn")
 
         def first_bank(name, n):
             return acc_psum.tile([P, N_TILE], F32, name=name, tag="acc%d" % n)
@@ -176,20 +185,20 @@ def tile_hadlinear_kernel(tc, x, weight_words, weight_scales, out):
 
         def transpose_unit(unit):
             words = x_chunk[unit][:].bitcast(F32)
-            t_bank = t_psum.tile([P, 4, P], F32, name="t_bank")
+            t_bank = bank_in_turn("t_bank")
             for pair in range(2):
                 for half in range(2):
                     nc.tensor.transpose(
-                        t_bank[:, 2 * pair + half, :],
+                        t_bank[:, P * (2 * pair + half) : P * (2 * pair + half + 1)],
                         words[:, 256 * half + pair : 256 * (half + 1) : 2],
                         identity[:],
                     )
             x_t[unit] = xt_pool.tile([P, BLOCK], BF16, name="x_t")
-            nc.scalar.copy(out=x_t[unit][:].bitcast(F32), in_=t_bank[:].rearrange("p s k -> p (s k)"))
+            nc.scalar.copy(out=x_t[unit][:].bitcast(F32), in_=t_bank[:])
 
         def hadamard_sum(unit):
             columns = x_t[unit][:].rearrange("p (w e) -> p w e", e=2)
-            z_sum = sum_psum.tile([P, 4 * P], F32, name="z_sum")
+            z_sum = bank_in_turn("z_sum")
             on_tensor = PLAIN_MATMULS[unit] >= 3
             nc.tensor.matmul(out=z_sum[:], lhsT=hadamard[:], rhs=columns[:, :, 0], start=True, stop=not on_tensor)
             if on_tensor:
@@ -262,36 +271,56 @@ def tile_hadlinear_kernel(tc, x, weight_words, weight_scales, out):
                 in_=grouped[unit][:].rearrange("p h k t -> p (h k t)"),
             )
 
-        def multiply(unit, side):
-            tile_index, block = divmod(unit, BLOCKS)
-            tiles_per_side = N_TILES // SIDES
-            for n in range(tiles_per_side * side, tiles_per_side * (side + 1)):
-                n_cols = slice(N_TILE * n, N_TILE * (n + 1))
-                side_cols = slice(N_TILE * (n % tiles_per_side), N_TILE * (n % tiles_per_side + 1))
-                if block == 0:
-                    acc[n] = acc_psum.tile([P, N_TILE], F32, name="acc%d" % n)
-                for half in range(2):
-                    g = 2 * block + half
-                    a, k = divmod(g, PLANES_PER_TILE)
-                    tokens = slice(P * half, P * (half + 1))
-                    nc.tensor.matmul_mx(
-                        out=acc[n][:],
-                        lhsT=y_codes[unit][:, tokens].bitcast(FP8X4),
-                        lhsT_scale=y_scales[unit][:, tokens],
-                        rhs=w_words[(g, side)][:, side_cols].bitcast(FP8X4),
-                        rhs_scale=w_planes[4 * k : P, a, n_cols],
-                        start=(g == 0),
-                        stop=(g == GROUPS - 1),
-                    )
-                if block == BLOCKS - 1:
+        def pieces_of(tile_index, side):
+            pieces = [(N_TILE * (tiles_per_side * side + i), N_TILE) for i in range(tiles_per_side)]
+            if (tile_index, side) == (TOKENS // P - 1, SIDES - 1):
+                first = pieces.pop()[0]
+                pieces += [(first, N_TILE // 2), (first + N_TILE // 2, N_TILE // 2)]
+            return pieces
+
+        def multiply(units, side):
+            tile_index = units[0] // BLOCKS
+            pieces = pieces_of(tile_index, side)
+            for i, (first_col, width) in enumerate(pieces):
+                for unit in units:
+                    multiply_piece(unit, side, i, first_col, width)
+                if units[-1] % BLOCKS == BLOCKS - 1:
                     result = store_pool.tile([P, N_TILE], F32, name="result")
-                    nc.scalar.copy(out=result[:], in_=acc[n][:])
-                    nc.sync.dma_start(out=out_rows[P * tile_index : P * (tile_index + 1), n_cols], in_=result[:])
+                    if len(pieces) > tiles_per_side and i == 1:
+                        nc.vector.tensor_copy(out=result[:, 0:width], in_=acc[(side, i)][:, 0:width])
+                    else:
+                        nc.scalar.copy(out=result[:, 0:width], in_=acc[(side, i)][:, 0:width])
+                    nc.sync.dma_start(
+                        out=out_rows[P * tile_index : P * (tile_index + 1), first_col : first_col + width],
+                        in_=result[:, 0:width],
+                    )
+
+        def multiply_piece(unit, side, i, first_col, width):
+            block = unit % BLOCKS
+            side_col = first_col - OUTPUTS // SIDES * side
+            if block == 0:
+                if i < tiles_per_side:
+                    acc[(side, i)] = acc_psum.tile([P, N_TILE], F32, name="acc", tag="acc%d" % (tiles_per_side * side + i))
+                else:
+                    acc[(side, i)] = bank_in_turn("acc_last")
+            for half in range(2):
+                g = 2 * block + half
+                a, k = divmod(g, PLANES_PER_TILE)
+                tokens = slice(P * half, P * (half + 1))
+                nc.tensor.matmul_mx(
+                    out=acc[(side, i)][:, 0:width],
+                    lhsT=y_codes[unit][:, tokens].bitcast(FP8X4),
+                    lhsT_scale=y_scales[unit][:, tokens],
+                    rhs=w_words[(g, side)][:, side_col : side_col + width].bitcast(FP8X4),
+                    rhs_scale=w_planes[4 * k : P, a, first_col : first_col + width],
+                    start=(g == 0),
+                    stop=(g == GROUPS - 1),
+                )
 
         def in_range(unit):
             return 0 <= unit < UNITS
 
-        for j in range(FIRST_STEP, UNITS + LEFT_BEHIND + RIGHT_LAG[-1]):
+        for j in range(FIRST_STEP, UNITS + LEFT_BEHIND):
             if j == FIRST_STEP:
                 start_first_unit()
             if in_range(j) and j > 0:
@@ -311,10 +340,14 @@ def tile_hadlinear_kernel(tc, x, weight_words, weight_scales, out):
             for unit in range(1, UNITS):
                 if unit - TRANSPOSE_AHEAD[unit] == j:
                     transpose_unit(unit)
-            if j == 0:
-                multiply(0, 0)
-            if in_range(j - LEFT_BEHIND) and j > LEFT_BEHIND:
-                multiply(j - LEFT_BEHIND, 0)
-            for unit in range(UNITS):
-                if unit + LEFT_BEHIND + RIGHT_LAG[unit] == j:
-                    multiply(unit, 1)
+            left = [0] if j == 0 else [u for u in range(1, UNITS) if u + LEFT_BEHIND == j]
+            right = [u for u in range(UNITS) if u + LEFT_BEHIND + RIGHT_LAG[u] == j]
+            passes = [(u, 0) for u in left] + [(u, 1) for u in right]
+            if j - LEFT_BEHIND >= W_LANDED:
+                passes = [(u, 1) for u in right] + [(u, 0) for u in left]
+            if j == UNITS:
+                multiply(left, 0)
+                multiply([u for u in range(UNITS) if u + LEFT_BEHIND + RIGHT_LAG[u] >= j], 1)
+                passes = []
+            for unit, side in passes:
+                multiply([unit], side)

@@ -70,7 +70,7 @@ def tile_hadlinear_kernel(tc, x, weight_words, weight_scales, out):
             )
 
         def load_w(g, side):
-            w_words[(g, side)] = w_pool.tile([P, OUTPUTS // SIDES], U32, name="w_words", align_bytes=64)
+            w_words[(g, side)] = w_pool.tile([P, OUTPUTS // SIDES], U32, name="w_words", align_bytes=256)
             side_bytes = 4 * OUTPUTS // SIDES
             nc.sync.dma_start(
                 out=w_words[(g, side)][:].bitcast(I32),
@@ -79,7 +79,7 @@ def tile_hadlinear_kernel(tc, x, weight_words, weight_scales, out):
                 .bitcast(I32),
             )
 
-        w_planes = const.tile([P, GROUPS // PLANES_PER_TILE, OUTPUTS], U8, align_bytes=64)
+        w_planes = const.tile([P, GROUPS // PLANES_PER_TILE, OUTPUTS], U8, align_bytes=256)
         nc.vector.memset(w_planes[:].rearrange("p a n -> p (a n)").bitcast(I32), 0)
 
         def load_scales(a):
@@ -253,7 +253,7 @@ def tile_hadlinear_kernel(tc, x, weight_words, weight_scales, out):
 
         def butterfly_half(unit):
             planes = after_pair[unit][:].rearrange("p u (h k) e -> p h k u e", h=2)
-            grouped[unit] = work.tile([P, 2, P, 4], BF16, name="grouped", align_bytes=64)
+            grouped[unit] = work.tile([P, 2, P, 4], BF16, name="grouped", align_bytes=256)
             for sign, op in enumerate((ALU.add, ALU.subtract)):
                 nc.vector.tensor_tensor(
                     out=grouped[unit][:, sign, :, :].rearrange("p k (u e) -> p k u e", u=2),
@@ -263,8 +263,8 @@ def tile_hadlinear_kernel(tc, x, weight_words, weight_scales, out):
                 )
 
         def quantise(unit):
-            y_codes[unit] = behind.tile([P, 2 * P], U32, name="y_codes", align_bytes=64)
-            y_scales[unit] = behind.tile([P, 2 * P], U8, name="y_scales", align_bytes=64)
+            y_codes[unit] = behind.tile([P, 2 * P], U32, name="y_codes", align_bytes=256)
+            y_scales[unit] = behind.tile([P, 2 * P], U8, name="y_scales", align_bytes=256)
             nc.vector.quantize_mx(
                 out=y_codes[unit][:].bitcast(FP8X4),
                 scales=y_scales[unit][:],

@@ -29,7 +29,8 @@ HADAMARD_AHEAD = 2
 X_AHEAD_OF_W = BLOCKS + 1
 TRANSPOSE_AHEAD = [4 if u < X_AHEAD_OF_W else 3 for u in range(UNITS)]
 FIRST_STEP = -3
-PLAIN_MATMULS = [4] * 7 + [2] * 5 + [3] * 4
+PLAIN_MATMULS = [4] * 7 + [2] * 9
+GPSIMD_TOKENS = {4: 0, 3: 0, 2: 96}
 LEFT_BEHIND = 1
 RIGHT_LAG = [max(2, min(4, 4 - (u - 3) // BLOCKS)) for u in range(UNITS)]
 W_LANDED = 2 * BLOCKS
@@ -251,14 +252,33 @@ def tile_hadlinear_kernel(tc, x, weight_words, weight_scales, out):
                     out=after_pair[unit][:, sign, :, :], in0=planes[:, 0, :, :], in1=planes[:, 1, :, :], op=op
                 )
 
-        def butterfly_half(unit):
-            planes = after_pair[unit][:].rearrange("p u (h k) e -> p h k u e", h=2)
+        def shared_tokens(unit):
+            return GPSIMD_TOKENS[PLAIN_MATMULS[unit + 1]] if unit + 1 < UNITS else 0
+
+        def half_planes(unit):
+            return after_pair[unit][:].rearrange("p u (h k) e -> p h k u e", h=2)
+
+        def butterfly_half_gpsimd(unit):
             grouped[unit] = work.tile([P, 2, P, 4], BF16, name="grouped", align_bytes=256)
+            if shared_tokens(unit) == 0:
+                return
+            planes = half_planes(unit)
+            tokens = slice(P - shared_tokens(unit), P)
+            nc.gpsimd.tensor_tensor(
+                out=grouped[unit][:, 1, tokens, :].rearrange("p k (u e) -> p k u e", u=2),
+                in0=planes[:, 0, tokens, :, :],
+                in1=planes[:, 1, tokens, :, :],
+                op=ALU.subtract,
+            )
+
+        def butterfly_half(unit):
+            planes = half_planes(unit)
             for sign, op in enumerate((ALU.add, ALU.subtract)):
+                tokens = slice(0, P - shared_tokens(unit) if sign else P)
                 nc.vector.tensor_tensor(
-                    out=grouped[unit][:, sign, :, :].rearrange("p k (u e) -> p k u e", u=2),
-                    in0=planes[:, 0, :, :, :],
-                    in1=planes[:, 1, :, :, :],
+                    out=grouped[unit][:, sign, tokens, :].rearrange("p k (u e) -> p k u e", u=2),
+                    in0=planes[:, 0, tokens, :, :],
+                    in1=planes[:, 1, tokens, :, :],
                     op=op,
                 )
 
@@ -323,6 +343,8 @@ def tile_hadlinear_kernel(tc, x, weight_words, weight_scales, out):
         for j in range(FIRST_STEP, UNITS + LEFT_BEHIND):
             if j == FIRST_STEP:
                 start_first_unit()
+            if in_range(j - 1) and j > 1:
+                butterfly_half_gpsimd(j - 1)
             if in_range(j) and j > 0:
                 difference_odd(j)
             if in_range(j - 1) and j > 1:
@@ -330,6 +352,7 @@ def tile_hadlinear_kernel(tc, x, weight_words, weight_scales, out):
             if in_range(j):
                 butterfly_pair(j)
             if j == 0:
+                butterfly_half_gpsimd(0)
                 butterfly_half(0)
                 quantise(0)
             if in_range(j - 1) and j > 1:

@@ -29,7 +29,7 @@ HADAMARD_AHEAD = 2
 X_AHEAD_OF_W = BLOCKS + 1
 TRANSPOSE_AHEAD = [4 if u < X_AHEAD_OF_W else 3 for u in range(UNITS)]
 FIRST_STEP = -3
-PLAIN_MATMULS = [4] * 7 + [2] * 9
+PLAIN_MATMULS = [4] * 6 + [2] * 10
 GPSIMD_TOKENS = {4: 0, 3: 0, 2: 96}
 LEFT_BEHIND = 1
 RIGHT_LAG = [max(2, min(4, 4 - (u - 3) // BLOCKS)) for u in range(UNITS)]
@@ -172,6 +172,7 @@ def tile_hadlinear_kernel(tc, x, weight_words, weight_scales, out):
                 nc.scalar.copy(
                     out=x_t[0][:, 4 * P * pair : 4 * P * (pair + 1)].bitcast(F32), in_=banks[pair][:, 0 : 2 * P]
                 )
+            transpose_unit(1)
             for pair in range(2):
                 cols = slice(2 * P * pair, 2 * P * (pair + 1))
                 z_sum = first_bank("first_sum", 2 * pair + 1)
@@ -306,7 +307,7 @@ def tile_hadlinear_kernel(tc, x, weight_words, weight_scales, out):
                     multiply_piece(unit, side, i, first_col, width)
                 if units[-1] % BLOCKS == BLOCKS - 1:
                     result = store_pool.tile([P, N_TILE], F32, name="result")
-                    if len(pieces) > tiles_per_side and i == 1:
+                    if len(pieces) > tiles_per_side and i == 2:
                         nc.vector.tensor_copy(out=result[:, 0:width], in_=acc[(side, i)][:, 0:width])
                     else:
                         nc.scalar.copy(out=result[:, 0:width], in_=acc[(side, i)][:, 0:width])
@@ -360,7 +361,7 @@ def tile_hadlinear_kernel(tc, x, weight_words, weight_scales, out):
             if in_range(j + HADAMARD_AHEAD) and j + HADAMARD_AHEAD > 0:
                 hadamard_sum(j + HADAMARD_AHEAD)
                 hadamard_odd(j + HADAMARD_AHEAD)
-            for unit in range(1, UNITS):
+            for unit in range(2, UNITS):
                 if unit - TRANSPOSE_AHEAD[unit] == j:
                     transpose_unit(unit)
             left = [0] if j == 0 else [u for u in range(1, UNITS) if u + LEFT_BEHIND == j]

@@ -28,14 +28,21 @@ SCALE = 1.0 / 32.0
 HADAMARD_AHEAD = 2
 X_AHEAD_OF_W = BLOCKS + 1
 TRANSPOSE_AHEAD = [4 if u < X_AHEAD_OF_W else 3 for u in range(UNITS)]
-FIRST_STEP = -3
-PLAIN_MATMULS = [4] * 6 + [2] * 10
-GPSIMD_TOKENS = {4: 0, 3: 0, 2: 96}
-LEFT_BEHIND = 1
-RIGHT_LAG = [max(2, min(4, 4 - (u - 3) // BLOCKS)) for u in range(UNITS)]
-W_LANDED = 2 * BLOCKS
+FIRST_STEP = -2
+PLAIN_MATMULS = [4] * 7 + [2] * 9
+GPSIMD_TOKENS = {4: 0, 2: 96}
+STREAMS = ((0, 2 * N_TILE), (2 * N_TILE, N_TILE), (3 * N_TILE, N_TILE))
+W_LANDED = 11
 WARM_UP = 4
-SIDES = 2
+
+
+def multiply_step(unit, stream):
+    if stream == 0:
+        return unit + 1 if unit > 0 else 0
+    if stream == 1:
+        return max(unit + 3, min(unit + 5, W_LANDED + 2))
+    return max(unit + 3, min(unit + 8, W_LANDED + unit // BLOCKS))
+
 
 FLOPS = 2 * TOKENS * FEATURES * OUTPUTS + 10 * TOKENS * FEATURES
 
@@ -47,17 +54,23 @@ def tile_hadlinear_kernel(tc, x, weight_words, weight_scales, out):
 
     with ExitStack() as ctx:
         const = ctx.enter_context(tc.tile_pool(name="const", bufs=1))
-        xt_pool = ctx.enter_context(tc.tile_pool(name="xt_pool", bufs=4))
         x_pool = ctx.enter_context(tc.tile_pool(name="x_pool", bufs=UNITS))
-        w_pool = ctx.enter_context(tc.tile_pool(name="w_pool", bufs=SIDES * GROUPS))
+        w_pool = ctx.enter_context(tc.tile_pool(name="w_pool", bufs=GROUPS))
+        xt_pool = ctx.enter_context(tc.tile_pool(name="xt_pool", bufs=4))
         work = ctx.enter_context(tc.tile_pool(name="work", bufs=2))
         ahead = ctx.enter_context(tc.tile_pool(name="ahead", bufs=HADAMARD_AHEAD + 2))
-        behind = ctx.enter_context(tc.tile_pool(name="behind", bufs=8))
+        behind = ctx.enter_context(tc.tile_pool(name="behind", bufs=11))
         store_pool = ctx.enter_context(tc.tile_pool(name="store_pool", bufs=2 * N_TILES))
         turn_psum = ctx.enter_context(tc.psum_pool(name="turn_psum", bufs=2))
         odd_psum = ctx.enter_context(tc.psum_pool(name="odd_psum", bufs=2))
         acc_psum = ctx.enter_context(tc.psum_pool(name="acc_psum", bufs=1))
         ctx.enter_context(tc.manual_schedule())
+
+        def bank_in_turn(name):
+            return turn_psum.tile([P, N_TILE], F32, name=name, tag="turn")
+
+        def acc_bank(name, n):
+            return acc_psum.tile([P, N_TILE], F32, name=name, tag="acc%d" % n)
 
         x_chunk = {}
         w_words = {}
@@ -70,14 +83,12 @@ def tile_hadlinear_kernel(tc, x, weight_words, weight_scales, out):
                 in_=x_rows[P * tile_index : P * (tile_index + 1), BLOCK * block : BLOCK * (block + 1)],
             )
 
-        def load_w(g, side):
-            w_words[(g, side)] = w_pool.tile([P, OUTPUTS // SIDES], U32, name="w_words", align_bytes=256)
-            side_bytes = 4 * OUTPUTS // SIDES
+        def load_w(g, stream):
+            first, width = STREAMS[stream]
+            w_words[(g, stream)] = w_pool.tile([P, width], U32, name="w_words_%d" % stream, align_bytes=256)
             nc.sync.dma_start(
-                out=w_words[(g, side)][:].bitcast(I32),
-                in_=weight_words[g]
-                .rearrange("p n t -> p (n t)")[:, side_bytes * side : side_bytes * (side + 1)]
-                .bitcast(I32),
+                out=w_words[(g, stream)][:].bitcast(I32),
+                in_=weight_words[g].rearrange("p n t -> p (n t)")[:, 4 * first : 4 * (first + width)].bitcast(I32),
             )
 
         w_planes = const.tile([P, GROUPS // PLANES_PER_TILE, OUTPUTS], U8, align_bytes=256)
@@ -91,18 +102,19 @@ def tile_hadlinear_kernel(tc, x, weight_words, weight_scales, out):
                         PLANES_PER_TILE * a : PLANES_PER_TILE * (a + 1), 4 * quadrant : 4 * quadrant + 4, :
                     ].bitcast(I32),
                 )
+
         for unit in range(X_AHEAD_OF_W):
             load_x(unit)
         load_scales(0)
-        for side in range(SIDES):
+        for stream in range(len(STREAMS)):
             for block in range(BLOCKS):
-                load_w(2 * block, side)
-                load_w(2 * block + 1, side)
-                if side == 0 and block == 1:
+                load_w(2 * block, stream)
+                load_w(2 * block + 1, stream)
+                if (stream, 2 * block) == (0, PLANES_PER_TILE):
                     load_scales(1)
-                load_x(X_AHEAD_OF_W + BLOCKS * side + block)
-        for unit in range(X_AHEAD_OF_W + BLOCKS * SIDES, UNITS):
-            load_x(unit)
+                unit = X_AHEAD_OF_W + BLOCKS * stream + block
+                if unit < UNITS:
+                    load_x(unit)
 
         warm = const.tile([P, 1], F32)
         nc.gpsimd.memset(warm[:], 0.0)
@@ -114,7 +126,7 @@ def tile_hadlinear_kernel(tc, x, weight_words, weight_scales, out):
         nc.gpsimd.iota(col_index[:], pattern=[[1, P]], base=0, channel_multiplier=0)
         zeros = const.tile([P, P], F32)
         nc.gpsimd.memset(zeros[:], 0.0)
-        warm_bank = acc_psum.tile([P, N_TILE], F32, name="warm_bank", tag="acc3")
+        warm_bank = acc_bank("warm_bank", 3)
         for _ in range(WARM_UP):
             nc.tensor.matmul(out=warm_bank[:, 0:P], lhsT=zeros[:], rhs=zeros[:], start=True, stop=True)
         identity = const.tile([P, P], F32)
@@ -149,139 +161,102 @@ def tile_hadlinear_kernel(tc, x, weight_words, weight_scales, out):
         y_codes = {}
         y_scales = {}
         acc = {}
-        tiles_per_side = N_TILES // SIDES
 
-        def bank_in_turn(name):
-            return turn_psum.tile([P, 4 * P], F32, name=name, tag="turn")
+        def transpose_words(unit, pair, half, out_cols):
+            words = x_chunk[unit][:].bitcast(F32)
+            nc.tensor.transpose(out_cols, words[:, 256 * half + pair : 256 * (half + 1) : 2], identity[:])
 
-        def first_bank(name, n):
-            return acc_psum.tile([P, N_TILE], F32, name=name, tag="acc%d" % n)
-
-        def start_first_unit():
-            words = x_chunk[0][:].bitcast(F32)
-            x_t[0] = xt_pool.tile([P, BLOCK], BF16, name="x_t")
-            after_odd[0] = ahead.tile([P, 2, 4 * P], F32, name="after_odd")
-            banks = [first_bank("first_t", 2 * pair) for pair in range(2)]
+        def transpose_unit(unit):
+            t_bank = bank_in_turn("t_bank")
             for pair in range(2):
                 for half in range(2):
-                    nc.tensor.transpose(
-                        banks[pair][:, P * half : P * (half + 1)],
-                        words[:, 256 * half + pair : 256 * (half + 1) : 2],
-                        identity[:],
-                    )
+                    slot = 2 * pair + half
+                    transpose_words(unit, pair, half, t_bank[:, P * slot : P * (slot + 1)])
+            x_t[unit] = xt_pool.tile([P, BLOCK], BF16, name="x_t")
+            nc.scalar.copy(out=x_t[unit][:].bitcast(F32), in_=t_bank[:])
+
+        def add_planes(out_cols, columns, second):
+            nc.tensor.matmul(out=out_cols, lhsT=hadamard[:], rhs=columns[:, :, 0], start=True, stop=False)
+            nc.tensor.matmul(out=out_cols, lhsT=second[:], rhs=columns[:, :, 1], start=False, stop=True)
+
+        def start_first_unit():
+            x_t[0] = xt_pool.tile([P, BLOCK], BF16, name="x_t")
+            after_odd[0] = ahead.tile([P, 2, 4 * P], F32, name="after_odd")
+            for pair in range(2):
+                t_bank = acc_bank("first_t", 2 * pair)
+                for half in range(2):
+                    transpose_words(0, pair, half, t_bank[:, P * half : P * (half + 1)])
                 nc.scalar.copy(
-                    out=x_t[0][:, 4 * P * pair : 4 * P * (pair + 1)].bitcast(F32), in_=banks[pair][:, 0 : 2 * P]
+                    out=x_t[0][:, 4 * P * pair : 4 * P * (pair + 1)].bitcast(F32), in_=t_bank[:, 0 : 2 * P]
                 )
             transpose_unit(1)
             for pair in range(2):
                 cols = slice(2 * P * pair, 2 * P * (pair + 1))
-                z_sum = first_bank("first_sum", 2 * pair + 1)
-                z_first = odd_psum.tile([P, 4 * P], F32, name="z_odd")
                 columns = x_t[0][:, 4 * P * pair : 4 * P * (pair + 1)].rearrange("p (w e) -> p w e", e=2)
-                nc.tensor.matmul(out=z_sum[:, 0 : 2 * P], lhsT=hadamard[:], rhs=columns[:, :, 0], start=True, stop=False)
-                nc.tensor.matmul(out=z_sum[:, 0 : 2 * P], lhsT=hadamard[:], rhs=columns[:, :, 1], start=False, stop=True)
+                z_sum = acc_bank("first_sum", 2 * pair + 1)
+                add_planes(z_sum[:, 0 : 2 * P], columns, hadamard)
                 nc.scalar.mul(out=after_odd[0][:, 0, cols], in_=z_sum[:, 0 : 2 * P], mul=SCALE)
-                nc.tensor.matmul(out=z_first[:, 0 : 2 * P], lhsT=hadamard[:], rhs=columns[:, :, 0], start=True, stop=False)
-                nc.tensor.matmul(out=z_first[:, 0 : 2 * P], lhsT=minus_hadamard[:], rhs=columns[:, :, 1], start=False, stop=True)
-                nc.vector.tensor_single_scalar(out=after_odd[0][:, 1, cols], in_=z_first[:, 0 : 2 * P], scalar=SCALE, op=ALU.mult)
+                z_difference = odd_psum.tile([P, 4 * P], F32, name="z_difference", tag="z_odd")
+                add_planes(z_difference[:, 0 : 2 * P], columns, minus_hadamard)
+                nc.vector.tensor_single_scalar(
+                    out=after_odd[0][:, 1, cols], in_=z_difference[:, 0 : 2 * P], scalar=SCALE, op=ALU.mult
+                )
 
-        def transpose_unit(unit):
-            words = x_chunk[unit][:].bitcast(F32)
-            t_bank = bank_in_turn("t_bank")
-            for pair in range(2):
-                for half in range(2):
-                    nc.tensor.transpose(
-                        t_bank[:, P * (2 * pair + half) : P * (2 * pair + half + 1)],
-                        words[:, 256 * half + pair : 256 * (half + 1) : 2],
-                        identity[:],
-                    )
-            x_t[unit] = xt_pool.tile([P, BLOCK], BF16, name="x_t")
-            nc.scalar.copy(out=x_t[unit][:].bitcast(F32), in_=t_bank[:])
-
-        def hadamard_sum(unit):
+        def hadamard_unit(unit):
             columns = x_t[unit][:].rearrange("p (w e) -> p w e", e=2)
-            z_sum = bank_in_turn("z_sum")
-            on_tensor = PLAIN_MATMULS[unit] >= 3
-            nc.tensor.matmul(out=z_sum[:], lhsT=hadamard[:], rhs=columns[:, :, 0], start=True, stop=not on_tensor)
-            if on_tensor:
-                nc.tensor.matmul(out=z_sum[:], lhsT=hadamard[:], rhs=columns[:, :, 1], start=False, stop=True)
-            after_odd[unit] = ahead.tile([P, 2, 4 * P], F32, name="after_odd")
-            if on_tensor:
-                nc.scalar.mul(out=after_odd[unit][:, 0, :], in_=z_sum[:], mul=SCALE)
-            else:
-                z_even[unit] = ahead.tile([P, 4 * P], F32, name="z_even")
-                nc.scalar.mul(out=z_even[unit][:], in_=z_sum[:], mul=SCALE)
-
-        def hadamard_odd(unit):
-            columns = x_t[unit][:].rearrange("p (w e) -> p w e", e=2)
+            bank = bank_in_turn("z_bank")
             z_odd[unit] = odd_psum.tile([P, 4 * P], F32, name="z_odd")
             if PLAIN_MATMULS[unit] == 4:
-                nc.tensor.matmul(out=z_odd[unit][:], lhsT=hadamard[:], rhs=columns[:, :, 0], start=True, stop=False)
-                nc.tensor.matmul(out=z_odd[unit][:], lhsT=minus_hadamard[:], rhs=columns[:, :, 1], start=False, stop=True)
-                nc.scalar.mul(out=after_odd[unit][:, 1, :], in_=z_odd[unit][:], mul=SCALE)
+                after_odd[unit] = ahead.tile([P, 2, 4 * P], F32, name="after_odd")
+                for odd, (z_bank, second) in enumerate(((bank, hadamard), (z_odd[unit], minus_hadamard))):
+                    add_planes(z_bank[:], columns, second)
+                    nc.scalar.mul(out=after_odd[unit][:, odd, :], in_=z_bank[:], mul=SCALE)
             else:
+                nc.tensor.matmul(out=bank[:], lhsT=hadamard[:], rhs=columns[:, :, 0], start=True, stop=True)
+                z_even[unit] = ahead.tile([P, 4 * P], F32, name="z_even")
+                nc.scalar.mul(out=z_even[unit][:], in_=bank[:], mul=SCALE)
                 nc.tensor.matmul(out=z_odd[unit][:], lhsT=hadamard[:], rhs=columns[:, :, 1], start=True, stop=True)
 
-        def difference_odd(unit):
-            if PLAIN_MATMULS[unit] == 4:
-                return
-            if PLAIN_MATMULS[unit] == 2:
-                for sign, scalar in enumerate((SCALE, -SCALE)):
-                    nc.vector.scalar_tensor_tensor(
-                        out=after_odd[unit][:, sign, :],
-                        in0=z_odd[unit][:],
-                        scalar=scalar,
-                        in1=z_even[unit][:],
-                        op0=ALU.mult,
-                        op1=ALU.add,
-                    )
-                return
-            nc.vector.scalar_tensor_tensor(
-                out=after_odd[unit][:, 1, :],
-                in0=z_odd[unit][:],
-                scalar=-2.0 * SCALE,
-                in1=after_odd[unit][:, 0, :],
-                op0=ALU.mult,
-                op1=ALU.add,
-            )
+        def butterfly_odd(unit):
+            after_odd[unit] = ahead.tile([P, 2, 4 * P], F32, name="after_odd")
+            for odd, scalar in enumerate((SCALE, -SCALE)):
+                nc.vector.scalar_tensor_tensor(
+                    out=after_odd[unit][:, odd, :],
+                    in0=z_odd[unit][:],
+                    scalar=scalar,
+                    in1=z_even[unit][:],
+                    op0=ALU.mult,
+                    op1=ALU.add,
+                )
 
         def butterfly_pair(unit):
             planes = after_odd[unit][:].rearrange("p e (u c) -> p u c e", u=2)
             after_pair[unit] = work.tile([P, 2, 2 * P, 2], F32, name="after_pair")
-            for sign, op in enumerate((ALU.add, ALU.subtract)):
+            for pair, op in enumerate((ALU.add, ALU.subtract)):
                 nc.vector.tensor_tensor(
-                    out=after_pair[unit][:, sign, :, :], in0=planes[:, 0, :, :], in1=planes[:, 1, :, :], op=op
+                    out=after_pair[unit][:, pair, :, :], in0=planes[:, 0, :, :], in1=planes[:, 1, :, :], op=op
                 )
 
-        def shared_tokens(unit):
-            return GPSIMD_TOKENS[PLAIN_MATMULS[unit + 1]] if unit + 1 < UNITS else 0
+        def butterfly_half(engine, unit, half, tokens):
+            planes = after_pair[unit][:].rearrange("p u (h k) e -> p h k u e", h=2)
+            engine.tensor_tensor(
+                out=grouped[unit][:, half, tokens, :].rearrange("p k (u e) -> p k u e", u=2),
+                in0=planes[:, 0, tokens, :, :],
+                in1=planes[:, 1, tokens, :, :],
+                op=(ALU.add, ALU.subtract)[half],
+            )
 
-        def half_planes(unit):
-            return after_pair[unit][:].rearrange("p u (h k) e -> p h k u e", h=2)
+        def gpsimd_tokens(unit):
+            return GPSIMD_TOKENS[PLAIN_MATMULS[unit + 1]] if unit + 1 < UNITS else 0
 
         def butterfly_half_gpsimd(unit):
             grouped[unit] = work.tile([P, 2, P, 4], BF16, name="grouped", align_bytes=256)
-            if shared_tokens(unit) == 0:
-                return
-            planes = half_planes(unit)
-            tokens = slice(P - shared_tokens(unit), P)
-            nc.gpsimd.tensor_tensor(
-                out=grouped[unit][:, 1, tokens, :].rearrange("p k (u e) -> p k u e", u=2),
-                in0=planes[:, 0, tokens, :, :],
-                in1=planes[:, 1, tokens, :, :],
-                op=ALU.subtract,
-            )
+            if gpsimd_tokens(unit) > 0:
+                butterfly_half(nc.gpsimd, unit, 1, slice(P - gpsimd_tokens(unit), P))
 
-        def butterfly_half(unit):
-            planes = half_planes(unit)
-            for sign, op in enumerate((ALU.add, ALU.subtract)):
-                tokens = slice(0, P - shared_tokens(unit) if sign else P)
-                nc.vector.tensor_tensor(
-                    out=grouped[unit][:, sign, tokens, :].rearrange("p k (u e) -> p k u e", u=2),
-                    in0=planes[:, 0, tokens, :, :],
-                    in1=planes[:, 1, tokens, :, :],
-                    op=op,
-                )
+        def butterfly_half_vector(unit):
+            butterfly_half(nc.vector, unit, 0, slice(0, P))
+            butterfly_half(nc.vector, unit, 1, slice(0, P - gpsimd_tokens(unit)))
 
         def quantise(unit):
             y_codes[unit] = behind.tile([P, 2 * P], U32, name="y_codes", align_bytes=256)
@@ -292,86 +267,80 @@ def tile_hadlinear_kernel(tc, x, weight_words, weight_scales, out):
                 in_=grouped[unit][:].rearrange("p h k t -> p (h k t)"),
             )
 
-        def pieces_of(tile_index, side):
-            pieces = [(N_TILE * (tiles_per_side * side + i), N_TILE) for i in range(tiles_per_side)]
-            if (tile_index, side) == (TOKENS // P - 1, SIDES - 1):
+        def pieces_of(tile_index, stream):
+            first, width = STREAMS[stream]
+            pieces = [(first + c, N_TILE) for c in range(0, width, N_TILE)]
+            if (tile_index, stream) == (TOKENS // P - 1, len(STREAMS) - 1):
                 first = pieces.pop()[0]
                 pieces += [(first, N_TILE // 2), (first + N_TILE // 2, N_TILE // 2)]
             return pieces
 
-        def multiply(units, side):
-            tile_index = units[0] // BLOCKS
-            pieces = pieces_of(tile_index, side)
-            for i, (first_col, width) in enumerate(pieces):
-                for unit in units:
-                    multiply_piece(unit, side, i, first_col, width)
-                if units[-1] % BLOCKS == BLOCKS - 1:
-                    result = store_pool.tile([P, N_TILE], F32, name="result")
-                    if len(pieces) > tiles_per_side and i == 2:
-                        nc.vector.tensor_copy(out=result[:, 0:width], in_=acc[(side, i)][:, 0:width])
-                    else:
-                        nc.scalar.copy(out=result[:, 0:width], in_=acc[(side, i)][:, 0:width])
-                    nc.sync.dma_start(
-                        out=out_rows[P * tile_index : P * (tile_index + 1), first_col : first_col + width],
-                        in_=result[:, 0:width],
-                    )
-
-        def multiply_piece(unit, side, i, first_col, width):
+        def multiply_piece(unit, stream, first_col, width):
             block = unit % BLOCKS
-            side_col = first_col - OUTPUTS // SIDES * side
+            col = first_col - STREAMS[stream][0]
             if block == 0:
-                if i < tiles_per_side:
-                    acc[(side, i)] = acc_psum.tile([P, N_TILE], F32, name="acc", tag="acc%d" % (tiles_per_side * side + i))
+                if first_col % N_TILE == 0:
+                    acc[first_col] = acc_bank("acc", first_col // N_TILE)
                 else:
-                    acc[(side, i)] = bank_in_turn("acc_last")
+                    acc[first_col] = bank_in_turn("acc_last_half")
             for half in range(2):
                 g = 2 * block + half
                 a, k = divmod(g, PLANES_PER_TILE)
                 tokens = slice(P * half, P * (half + 1))
                 nc.tensor.matmul_mx(
-                    out=acc[(side, i)][:, 0:width],
+                    out=acc[first_col][:, 0:width],
                     lhsT=y_codes[unit][:, tokens].bitcast(FP8X4),
                     lhsT_scale=y_scales[unit][:, tokens],
-                    rhs=w_words[(g, side)][:, side_col : side_col + width].bitcast(FP8X4),
+                    rhs=w_words[(g, stream)][:, col : col + width].bitcast(FP8X4),
                     rhs_scale=w_planes[4 * k : P, a, first_col : first_col + width],
                     start=(g == 0),
                     stop=(g == GROUPS - 1),
                 )
 
+        def multiply(units, stream):
+            tile_index = units[0] // BLOCKS
+            for first_col, width in pieces_of(tile_index, stream):
+                for unit in units:
+                    multiply_piece(unit, stream, first_col, width)
+                if units[-1] % BLOCKS == BLOCKS - 1:
+                    result = store_pool.tile([P, N_TILE], F32, name="result")
+                    is_last = width < N_TILE and first_col + width == OUTPUTS
+                    copy = nc.vector.tensor_copy if is_last else nc.scalar.copy
+                    copy(out=result[:, 0:width], in_=acc[first_col][:, 0:width])
+                    nc.sync.dma_start(
+                        out=out_rows[P * tile_index : P * (tile_index + 1), first_col : first_col + width],
+                        in_=result[:, 0:width],
+                    )
+
         def in_range(unit):
             return 0 <= unit < UNITS
 
-        for j in range(FIRST_STEP, UNITS + LEFT_BEHIND):
-            if j == FIRST_STEP:
-                start_first_unit()
+        start_first_unit()
+        for j in range(FIRST_STEP, UNITS + 1):
             if in_range(j - 1) and j > 1:
                 butterfly_half_gpsimd(j - 1)
-            if in_range(j) and j > 0:
-                difference_odd(j)
+            if in_range(j) and PLAIN_MATMULS[j] == 2:
+                butterfly_odd(j)
             if in_range(j - 1) and j > 1:
-                butterfly_half(j - 1)
+                butterfly_half_vector(j - 1)
             if in_range(j):
                 butterfly_pair(j)
             if j == 0:
                 butterfly_half_gpsimd(0)
-                butterfly_half(0)
+                butterfly_half_vector(0)
                 quantise(0)
             if in_range(j - 1) and j > 1:
                 quantise(j - 1)
             if in_range(j + HADAMARD_AHEAD) and j + HADAMARD_AHEAD > 0:
-                hadamard_sum(j + HADAMARD_AHEAD)
-                hadamard_odd(j + HADAMARD_AHEAD)
+                hadamard_unit(j + HADAMARD_AHEAD)
             for unit in range(2, UNITS):
                 if unit - TRANSPOSE_AHEAD[unit] == j:
                     transpose_unit(unit)
-            left = [0] if j == 0 else [u for u in range(1, UNITS) if u + LEFT_BEHIND == j]
-            right = [u for u in range(UNITS) if u + LEFT_BEHIND + RIGHT_LAG[u] == j]
-            passes = [(u, 0) for u in left] + [(u, 1) for u in right]
-            if j - LEFT_BEHIND >= W_LANDED:
-                passes = [(u, 1) for u in right] + [(u, 0) for u in left]
-            if j == UNITS:
-                multiply(left, 0)
-                multiply([u for u in range(UNITS) if u + LEFT_BEHIND + RIGHT_LAG[u] >= j], 1)
-                passes = []
-            for unit, side in passes:
-                multiply([unit], side)
+            if j < UNITS:
+                for stream in (1, 0, 2) if j < W_LANDED else (2, 1, 0):
+                    for unit in range(UNITS):
+                        if multiply_step(unit, stream) == j:
+                            multiply([unit], stream)
+            else:
+                for stream in range(len(STREAMS)):
+                    multiply([u for u in range(UNITS) if multiply_step(u, stream) >= j], stream)

from contextlib import ExitStack

import concourse.masks as masks
import concourse.mybir as mybir

F32 = mybir.dt.float32
BF16 = mybir.dt.bfloat16
I32 = mybir.dt.int32
U32 = mybir.dt.uint32
U8 = mybir.dt.uint8
FP8X4 = mybir.dt.float8_e4m3fn_x4
ALU = mybir.AluOpType

P = 128
TOKENS = 512
FEATURES = 4096
OUTPUTS = 2048
BLOCK = 1024
K_PASS = 512
GROUPS = FEATURES // K_PASS
N_TILE = 512
N_TILES = OUTPUTS // N_TILE
BLOCKS = FEATURES // BLOCK
UNITS = (TOKENS // P) * BLOCKS
PLANES_PER_TILE = 4
SCALE = 1.0 / 32.0

HADAMARD_AHEAD = 2
X_AHEAD_OF_W = BLOCKS + 1
TRANSPOSE_AHEAD = [4 if u < X_AHEAD_OF_W else 3 for u in range(UNITS)]
FIRST_STEP = -2
PLAIN_MATMULS = [4] * 7 + [2] * 9
GPSIMD_TOKENS = {4: 0, 2: 96}
STREAMS = ((0, 2 * N_TILE), (2 * N_TILE, N_TILE), (3 * N_TILE, N_TILE))
W_LANDED = 11
WARM_UP = 4


def multiply_step(unit, stream):
    if stream == 0:
        return unit + 1 if unit > 0 else 0
    if stream == 1:
        return max(unit + 3, min(unit + 5, W_LANDED + 2))
    return max(unit + 3, min(unit + 8, W_LANDED + unit // BLOCKS))


FLOPS = 2 * TOKENS * FEATURES * OUTPUTS + 10 * TOKENS * FEATURES


def tile_hadlinear_kernel(tc, x, weight_words, weight_scales, out):
    nc = tc.nc
    x_rows = x.flatten_outer_dims()
    out_rows = out.flatten_outer_dims()

    with ExitStack() as ctx:
        const = ctx.enter_context(tc.tile_pool(name="const", bufs=1))
        x_pool = ctx.enter_context(tc.tile_pool(name="x_pool", bufs=UNITS))
        w_pool = ctx.enter_context(tc.tile_pool(name="w_pool", bufs=GROUPS))
        xt_pool = ctx.enter_context(tc.tile_pool(name="xt_pool", bufs=4))
        work = ctx.enter_context(tc.tile_pool(name="work", bufs=2))
        ahead = ctx.enter_context(tc.tile_pool(name="ahead", bufs=HADAMARD_AHEAD + 2))
        behind = ctx.enter_context(tc.tile_pool(name="behind", bufs=11))
        store_pool = ctx.enter_context(tc.tile_pool(name="store_pool", bufs=2 * N_TILES))
        turn_psum = ctx.enter_context(tc.psum_pool(name="turn_psum", bufs=2))
        odd_psum = ctx.enter_context(tc.psum_pool(name="odd_psum", bufs=2))
        acc_psum = ctx.enter_context(tc.psum_pool(name="acc_psum", bufs=1))
        ctx.enter_context(tc.manual_schedule())

        def bank_in_turn(name):
            return turn_psum.tile([P, N_TILE], F32, name=name, tag="turn")

        def acc_bank(name, n):
            return acc_psum.tile([P, N_TILE], F32, name=name, tag="acc%d" % n)

        x_chunk = {}
        w_words = {}

        def load_x(unit):
            tile_index, block = divmod(unit, BLOCKS)
            x_chunk[unit] = x_pool.tile([P, BLOCK], BF16, name="x_chunk")
            nc.sync.dma_start(
                out=x_chunk[unit][:],
                in_=x_rows[P * tile_index : P * (tile_index + 1), BLOCK * block : BLOCK * (block + 1)],
            )

        def load_w(g, stream):
            first, width = STREAMS[stream]
            w_words[(g, stream)] = w_pool.tile([P, width], U32, name="w_words_%d" % stream, align_bytes=256)
            nc.sync.dma_start(
                out=w_words[(g, stream)][:].bitcast(I32),
                in_=weight_words[g].rearrange("p n t -> p (n t)")[:, 4 * first : 4 * (first + width)].bitcast(I32),
            )

        w_planes = const.tile([P, GROUPS // PLANES_PER_TILE, OUTPUTS], U8, align_bytes=256)
        nc.vector.memset(w_planes[:].rearrange("p a n -> p (a n)").bitcast(I32), 0)

        def load_scales(a):
            for quadrant in range(4):
                nc.sync.dma_start(
                    out=w_planes[32 * quadrant : 32 * quadrant + 16, a, :].bitcast(I32),
                    in_=weight_scales[
                        PLANES_PER_TILE * a : PLANES_PER_TILE * (a + 1), 4 * quadrant : 4 * quadrant + 4, :
                    ].bitcast(I32),
                )

        for unit in range(X_AHEAD_OF_W):
            load_x(unit)
        load_scales(0)
        for stream in range(len(STREAMS)):
            for block in range(BLOCKS):
                load_w(2 * block, stream)
                load_w(2 * block + 1, stream)
                if (stream, 2 * block) == (0, PLANES_PER_TILE):
                    load_scales(1)
                unit = X_AHEAD_OF_W + BLOCKS * stream + block
                if unit < UNITS:
                    load_x(unit)

        warm = const.tile([P, 1], F32)
        nc.gpsimd.memset(warm[:], 0.0)
        nc.scalar.mul(out=warm[:], in_=warm[:], mul=SCALE)

        row_index = const.tile([P, P], I32)
        col_index = const.tile([P, P], I32)
        nc.gpsimd.iota(row_index[:], pattern=[[0, P]], base=0, channel_multiplier=1)
        nc.gpsimd.iota(col_index[:], pattern=[[1, P]], base=0, channel_multiplier=0)
        zeros = const.tile([P, P], F32)
        nc.gpsimd.memset(zeros[:], 0.0)
        warm_bank = acc_bank("warm_bank", 3)
        for _ in range(WARM_UP):
            nc.tensor.matmul(out=warm_bank[:, 0:P], lhsT=zeros[:], rhs=zeros[:], start=True, stop=True)
        identity = const.tile([P, P], F32)
        masks.make_identity(nc, identity[:])
        bits = const.tile([P, P], I32)
        nc.vector.tensor_tensor(out=bits[:], in0=row_index[:], in1=col_index[:], op=ALU.bitwise_and)
        for shift in (4, 2, 1):
            nc.vector.scalar_tensor_tensor(
                out=bits[:],
                in0=bits[:],
                scalar=shift,
                in1=bits[:],
                op0=ALU.logical_shift_right,
                op1=ALU.bitwise_xor,
            )
        nc.vector.tensor_single_scalar(out=bits[:], in_=bits[:], scalar=1, op=ALU.bitwise_and)
        hadamard = const.tile([P, P], BF16)
        nc.vector.tensor_scalar(
            out=hadamard[:], in0=bits[:], scalar1=-2.0, scalar2=1.0, op0=ALU.mult, op1=ALU.add
        )
        minus_hadamard = const.tile([P, P], BF16)
        nc.vector.tensor_scalar(
            out=minus_hadamard[:], in0=bits[:], scalar1=2.0, scalar2=-1.0, op0=ALU.mult, op1=ALU.add
        )

        x_t = {}
        z_odd = {}
        z_even = {}
        after_odd = {}
        after_pair = {}
        grouped = {}
        y_codes = {}
        y_scales = {}
        acc = {}

        def transpose_words(unit, pair, half, out_cols):
            words = x_chunk[unit][:].bitcast(F32)
            nc.tensor.transpose(out_cols, words[:, 256 * half + pair : 256 * (half + 1) : 2], identity[:])

        def transpose_unit(unit):
            t_bank = bank_in_turn("t_bank")
            for pair in range(2):
                for half in range(2):
                    slot = 2 * pair + half
                    transpose_words(unit, pair, half, t_bank[:, P * slot : P * (slot + 1)])
            x_t[unit] = xt_pool.tile([P, BLOCK], BF16, name="x_t")
            nc.scalar.copy(out=x_t[unit][:].bitcast(F32), in_=t_bank[:])

        def add_planes(out_cols, columns, second):
            nc.tensor.matmul(out=out_cols, lhsT=hadamard[:], rhs=columns[:, :, 0], start=True, stop=False)
            nc.tensor.matmul(out=out_cols, lhsT=second[:], rhs=columns[:, :, 1], start=False, stop=True)

        def start_first_unit():
            x_t[0] = xt_pool.tile([P, BLOCK], BF16, name="x_t")
            after_odd[0] = ahead.tile([P, 2, 4 * P], F32, name="after_odd")
            for pair in range(2):
                t_bank = acc_bank("first_t", 2 * pair)
                for half in range(2):
                    transpose_words(0, pair, half, t_bank[:, P * half : P * (half + 1)])
                nc.scalar.copy(
                    out=x_t[0][:, 4 * P * pair : 4 * P * (pair + 1)].bitcast(F32), in_=t_bank[:, 0 : 2 * P]
                )
            transpose_unit(1)
            for pair in range(2):
                cols = slice(2 * P * pair, 2 * P * (pair + 1))
                columns = x_t[0][:, 4 * P * pair : 4 * P * (pair + 1)].rearrange("p (w e) -> p w e", e=2)
                z_sum = acc_bank("first_sum", 2 * pair + 1)
                add_planes(z_sum[:, 0 : 2 * P], columns, hadamard)
                nc.scalar.mul(out=after_odd[0][:, 0, cols], in_=z_sum[:, 0 : 2 * P], mul=SCALE)
                z_difference = odd_psum.tile([P, 4 * P], F32, name="z_difference", tag="z_odd")
                add_planes(z_difference[:, 0 : 2 * P], columns, minus_hadamard)
                nc.vector.tensor_single_scalar(
                    out=after_odd[0][:, 1, cols], in_=z_difference[:, 0 : 2 * P], scalar=SCALE, op=ALU.mult
                )

        def hadamard_unit(unit):
            columns = x_t[unit][:].rearrange("p (w e) -> p w e", e=2)
            bank = bank_in_turn("z_bank")
            z_odd[unit] = odd_psum.tile([P, 4 * P], F32, name="z_odd")
            if PLAIN_MATMULS[unit] == 4:
                after_odd[unit] = ahead.tile([P, 2, 4 * P], F32, name="after_odd")
                for odd, (z_bank, second) in enumerate(((bank, hadamard), (z_odd[unit], minus_hadamard))):
                    add_planes(z_bank[:], columns, second)
                    nc.scalar.mul(out=after_odd[unit][:, odd, :], in_=z_bank[:], mul=SCALE)
            else:
                nc.tensor.matmul(out=bank[:], lhsT=hadamard[:], rhs=columns[:, :, 0], start=True, stop=True)
                z_even[unit] = ahead.tile([P, 4 * P], F32, name="z_even")
                nc.scalar.mul(out=z_even[unit][:], in_=bank[:], mul=SCALE)
                nc.tensor.matmul(out=z_odd[unit][:], lhsT=hadamard[:], rhs=columns[:, :, 1], start=True, stop=True)

        def butterfly_odd(unit):
            after_odd[unit] = ahead.tile([P, 2, 4 * P], F32, name="after_odd")
            for odd, scalar in enumerate((SCALE, -SCALE)):
                nc.vector.scalar_tensor_tensor(
                    out=after_odd[unit][:, odd, :],
                    in0=z_odd[unit][:],
                    scalar=scalar,
                    in1=z_even[unit][:],
                    op0=ALU.mult,
                    op1=ALU.add,
                )

        def butterfly_pair(unit):
            planes = after_odd[unit][:].rearrange("p e (u c) -> p u c e", u=2)
            after_pair[unit] = work.tile([P, 2, 2 * P, 2], F32, name="after_pair")
            for pair, op in enumerate((ALU.add, ALU.subtract)):
                nc.vector.tensor_tensor(
                    out=after_pair[unit][:, pair, :, :], in0=planes[:, 0, :, :], in1=planes[:, 1, :, :], op=op
                )

        def butterfly_half(engine, unit, half, tokens):
            planes = after_pair[unit][:].rearrange("p u (h k) e -> p h k u e", h=2)
            engine.tensor_tensor(
                out=grouped[unit][:, half, tokens, :].rearrange("p k (u e) -> p k u e", u=2),
                in0=planes[:, 0, tokens, :, :],
                in1=planes[:, 1, tokens, :, :],
                op=(ALU.add, ALU.subtract)[half],
            )

        def gpsimd_tokens(unit):
            return GPSIMD_TOKENS[PLAIN_MATMULS[unit + 1]] if unit + 1 < UNITS else 0

        def butterfly_half_gpsimd(unit):
            grouped[unit] = work.tile([P, 2, P, 4], BF16, name="grouped", align_bytes=256)
            if gpsimd_tokens(unit) > 0:
                butterfly_half(nc.gpsimd, unit, 1, slice(P - gpsimd_tokens(unit), P))

        def butterfly_half_vector(unit):
            butterfly_half(nc.vector, unit, 0, slice(0, P))
            butterfly_half(nc.vector, unit, 1, slice(0, P - gpsimd_tokens(unit)))

        def quantise(unit):
            y_codes[unit] = behind.tile([P, 2 * P], U32, name="y_codes", align_bytes=256)
            y_scales[unit] = behind.tile([P, 2 * P], U8, name="y_scales", align_bytes=256)
            nc.vector.quantize_mx(
                out=y_codes[unit][:].bitcast(FP8X4),
                scales=y_scales[unit][:],
                in_=grouped[unit][:].rearrange("p h k t -> p (h k t)"),
            )

        def pieces_of(tile_index, stream):
            first, width = STREAMS[stream]
            pieces = [(first + c, N_TILE) for c in range(0, width, N_TILE)]
            if (tile_index, stream) == (TOKENS // P - 1, len(STREAMS) - 1):
                first = pieces.pop()[0]
                pieces += [(first, N_TILE // 2), (first + N_TILE // 2, N_TILE // 2)]
            return pieces

        def multiply_piece(unit, stream, first_col, width):
            block = unit % BLOCKS
            col = first_col - STREAMS[stream][0]
            if block == 0:
                if first_col % N_TILE == 0:
                    acc[first_col] = acc_bank("acc", first_col // N_TILE)
                else:
                    acc[first_col] = bank_in_turn("acc_last_half")
            for half in range(2):
                g = 2 * block + half
                a, k = divmod(g, PLANES_PER_TILE)
                tokens = slice(P * half, P * (half + 1))
                nc.tensor.matmul_mx(
                    out=acc[first_col][:, 0:width],
                    lhsT=y_codes[unit][:, tokens].bitcast(FP8X4),
                    lhsT_scale=y_scales[unit][:, tokens],
                    rhs=w_words[(g, stream)][:, col : col + width].bitcast(FP8X4),
                    rhs_scale=w_planes[4 * k : P, a, first_col : first_col + width],
                    start=(g == 0),
                    stop=(g == GROUPS - 1),
                )

        def multiply(units, stream):
            tile_index = units[0] // BLOCKS
            for first_col, width in pieces_of(tile_index, stream):
                for unit in units:
                    multiply_piece(unit, stream, first_col, width)
                if units[-1] % BLOCKS == BLOCKS - 1:
                    result = store_pool.tile([P, N_TILE], F32, name="result")
                    is_last = width < N_TILE and first_col + width == OUTPUTS
                    copy = nc.vector.tensor_copy if is_last else nc.scalar.copy
                    copy(out=result[:, 0:width], in_=acc[first_col][:, 0:width])
                    nc.sync.dma_start(
                        out=out_rows[P * tile_index : P * (tile_index + 1), first_col : first_col + width],
                        in_=result[:, 0:width],
                    )

        def in_range(unit):
            return 0 <= unit < UNITS

        start_first_unit()
        for j in range(FIRST_STEP, UNITS + 1):
            if in_range(j - 1) and j > 1:
                butterfly_half_gpsimd(j - 1)
            if in_range(j) and PLAIN_MATMULS[j] == 2:
                butterfly_odd(j)
            if in_range(j - 1) and j > 1:
                butterfly_half_vector(j - 1)
            if in_range(j):
                butterfly_pair(j)
            if j == 0:
                butterfly_half_gpsimd(0)
                butterfly_half_vector(0)
                quantise(0)
            if in_range(j - 1) and j > 1:
                quantise(j - 1)
            if in_range(j + HADAMARD_AHEAD) and j + HADAMARD_AHEAD > 0:
                hadamard_unit(j + HADAMARD_AHEAD)
            for unit in range(2, UNITS):
                if unit - TRANSPOSE_AHEAD[unit] == j:
                    transpose_unit(unit)
            if j < UNITS:
                for stream in (1, 0, 2) if j < W_LANDED else (2, 1, 0):
                    for unit in range(UNITS):
                        if multiply_step(unit, stream) == j:
                            multiply([unit], stream)
            else:
                for stream in range(len(STREAMS)):
                    multiply([u for u in range(UNITS) if multiply_step(u, stream) >= j], stream)
